import numpy as np
import ml_dtypes


def mxq(x, axis, fmt="e4m3"):
    dtype, down = {"e4m3": (ml_dtypes.float8_e4m3fn, 7), "e5m2": (ml_dtypes.float8_e5m2, 14)}[fmt]
    v = np.moveaxis(np.asarray(x, np.float32).astype(ml_dtypes.bfloat16).astype(np.float64), axis, -1)
    blocks = v.reshape(v.shape[:-1] + (-1, 32))
    amax = np.abs(blocks).max(-1, keepdims=True)
    byte = np.maximum(np.where(amax > 0, np.frexp(amax)[1] - 1 + 127, 0) - down, 1)
    scale = np.exp2(byte - 127.0)
    codes = (blocks / scale).astype(np.float32).astype(dtype).astype(np.float64)
    return np.moveaxis((codes * scale).reshape(v.shape), -1, axis)


WIDE = False


def mx_kscale(k):
    if not WIDE:
        return np.ones(k)
    levels = np.array([10, -10, 5, -5, 0])
    a = np.random.permutation(np.resize(levels, k // 512 * 4)).reshape(k // 512, 4)
    idx = np.arange(k)
    return np.exp2(a[idx // 512, idx % 128 // 32])


BF16 = ml_dtypes.bfloat16


def bf(x):
    return np.asarray(x, np.float32).astype(BF16)


def f64(x):
    return np.asarray(x).astype(np.float64)


N, M, P, D = 8192, 512, 256, 16
LN_EPS = 1e-5
LENGTHSCALE = 1.0
INPUT_LB, INPUT_UB = -2.0, 2.0


def setup_inputs():
    s = mx_kscale(M)
    r = s.max() / s
    c = np.random.standard_normal(D)
    c = (c - c.mean()) / c.std()
    x = c + np.random.standard_normal((N, D)) * 1.6 / D
    z = c + np.random.uniform(INPUT_LB, INPUT_UB, (M, D)) * 1.6 / D
    z[:, 0] += np.log(r) * LENGTHSCALE
    g = np.random.standard_normal((M, P)) * 4.0 / np.sqrt(M)
    w = np.triu(g) + 0.1 * np.tril(g, -1) + np.eye(M, P)
    return {"x": bf(x), "design_points": bf(z), "chol_inv": bf(w * r[:, None])}


def reference(x, design_points, chol_inv):
    x, z = f64(x), f64(design_points)
    mean = np.mean(x, axis=-1, keepdims=True)
    var = np.mean(np.square(x - mean), axis=-1, keepdims=True)
    xn = (x - mean) / np.sqrt(var + LN_EPS)
    l1 = np.zeros((N, M))
    for d in range(D):
        l1 = l1 + np.abs(xn[:, d, None] - z[None, :, d])
    kmat = np.exp(-l1 / LENGTHSCALE)
    return mxq(kmat, 1, "e4m3") @ mxq(f64(chol_inv), 0, "e4m3")

@@ -1,0 +1,163 @@
+from contextlib import ExitStack
+
+import concourse.mybir as mybir
+from concourse.masks import make_identity
+
+F32 = mybir.dt.float32
+BF16 = mybir.dt.bfloat16
+U32 = mybir.dt.uint32
+U8 = mybir.dt.uint8
+FP8X4 = mybir.dt.float8_e4m3fn_x4
+ALU = mybir.AluOpType
+ACT = mybir.ActivationFunctionType
+AX = mybir.AxisListType
+
+N, M, POUT, D = 8192, 512, 256, 16
+P = 128
+NT = N // P
+PACK = 4
+LN_EPS = 1e-5
+BIG = 3.0e38
+FLOPS = 2 * N * M * POUT
+
+NS = 5
+NG = 5
+NV = 6
+QB = 4
+
+
+def tile_tmk_t_kernel(tc, x, design_points, chol_inv, out):
+    nc = tc.nc
+    nsb = NS + NG
+    with ExitStack() as ctx:
+        const = ctx.enter_context(tc.tile_pool(name="const", bufs=1))
+        tsp = ctx.enter_context(tc.tile_pool(name="tsp", bufs=3))
+        tgp = ctx.enter_context(tc.tile_pool(name="tgp", bufs=3))
+        tvp = ctx.enter_context(tc.tile_pool(name="tvp", bufs=4))
+        kqp = ctx.enter_context(tc.tile_pool(name="kqp", bufs=3))
+        cqp = ctx.enter_context(tc.tile_pool(name="cqp", bufs=3))
+        osp = ctx.enter_context(tc.tile_pool(name="osp", bufs=3))
+        psz = ctx.enter_context(tc.psum_pool(name="psz", bufs=1))
+        psa = ctx.enter_context(tc.psum_pool(name="psa", bufs=3))
+        pso = ctx.enter_context(tc.psum_pool(name="pso", bufs=2))
+
+        x_sb = const.tile([P, NT, D], BF16)
+        nc.sync.dma_start(out=x_sb[:], in_=x.rearrange("(p i) d -> p i d", i=NT))
+        z_sb = const.tile([P, PACK, D], BF16)
+        nc.sync.dma_start(out=z_sb[:], in_=design_points.rearrange("(p t) d -> p t d", t=PACK))
+        w_raw = const.tile([P, PACK, POUT], BF16)
+        nc.sync.dma_start(out=w_raw[:], in_=chol_inv.rearrange("(p j) w -> p j w", j=PACK))
+
+        ident_f = const.tile([P, P], F32)
+        make_identity(nc, ident_f[:])
+        ident_b = const.tile([P, P], BF16)
+        make_identity(nc, ident_b[:])
+
+        zb = const.tile([P, nsb, M], BF16)
+        for pair in range(nsb // 2):
+            tp = psa.tile([P, 2 * M], BF16, tag="acc")
+            for h in range(2):
+                d = 2 * pair + h
+                for t in range(PACK):
+                    c0 = h * M + t * P
+                    nc.tensor.transpose(tp[:, c0:c0 + P], z_sb[:, t, d:d + 1].to_broadcast([P, P]), ident_b[:])
+            nc.scalar.copy(out=zb[:, 2 * pair:2 * pair + 2, :], in_=tp[:].rearrange("p (h m) -> p h m", h=2))
+        zps = []
+        for b in range(NV // 2):
+            zp = psz.tile([P, 2 * M], BF16, name="zp%d" % b)
+            for h in range(2):
+                d = D - NV + 2 * b + h
+                for t in range(PACK):
+                    c0 = h * M + t * P
+                    nc.tensor.transpose(zp[:, c0:c0 + P], z_sb[:, t, d:d + 1].to_broadcast([P, P]), ident_b[:])
+            zps.append(zp)
+
+        zf = const.tile([P, PACK, D], F32)
+        nc.vector.tensor_copy(out=zf[:], in_=z_sb[:])
+        s_all = const.tile([P, PACK], F32)
+        nc.vector.tensor_reduce(out=s_all[:], in_=zf[:], axis=AX.X, op=ALU.add)
+        s_sc = const.tile([P, PACK], F32)
+        nc.vector.tensor_reduce(out=s_sc[:], in_=zf[:, :, 0:NS], axis=AX.X, op=ALU.add)
+        cz = const.tile([P, PACK], F32)
+        nc.vector.scalar_tensor_tensor(out=cz[:], in0=s_all[:], scalar=-0.5, in1=s_sc[:], op0=ALU.mult, op1=ALU.add)
+        cp = psa.tile([P, M], F32, tag="acc")
+        for t in range(PACK):
+            nc.tensor.transpose(cp[:, t * P:(t + 1) * P], cz[:, t:t + 1].to_broadcast([P, P]), ident_f[:])
+        c_sb = const.tile([P, M], F32)
+        nc.vector.tensor_copy(out=c_sb[:], in_=cp[:])
+
+        w_grp = const.tile([P, POUT, PACK], BF16, align_bytes=64)
+        nc.vector.tensor_copy(out=w_grp[:], in_=w_raw[:].rearrange("p j w -> p w j"))
+        w_codes = const.tile([P, POUT], U32, align_bytes=64)
+        w_scl = const.tile([P, POUT], U8, align_bytes=64)
+
+        xf = const.tile([P, NT, D], F32)
+        nc.vector.tensor_copy(out=xf[:], in_=x_sb[:])
+        mean = const.tile([P, NT], F32)
+        nc.vector.tensor_reduce(out=mean[:], in_=xf[:], axis=AX.X, op=ALU.add)
+        nc.vector.tensor_scalar(out=mean[:], in0=mean[:], scalar1=1.0 / D, scalar2=None, op0=ALU.mult)
+        xc = const.tile([P, NT, D], F32)
+        nc.vector.tensor_tensor(out=xc[:], in0=xf[:], in1=mean[:].unsqueeze(2).to_broadcast([P, NT, D]), op=ALU.subtract)
+        sq = const.tile([P, NT, D], F32)
+        nc.vector.tensor_tensor(out=sq[:], in0=xc[:], in1=xc[:], op=ALU.mult)
+        ve = const.tile([P, NT], F32)
+        nc.vector.tensor_reduce(out=ve[:], in_=sq[:], axis=AX.X, op=ALU.add)
+        nc.vector.tensor_scalar(out=ve[:], in0=ve[:], scalar1=1.0 / D, scalar2=LN_EPS, op0=ALU.mult, op1=ALU.add)
+        sd = const.tile([P, NT], F32)
+        nc.scalar.activation(out=sd[:], in_=ve[:], func=ACT.Sqrt)
+        rs = const.tile([P, NT], F32)
+        nc.vector.reciprocal(out=rs[:], in_=sd[:])
+        nw = const.tile([P, NT], F32)
+        nc.vector.tensor_tensor(out=nw[:], in0=rs[:], in1=rs[:], op=ALU.mult)
+        nc.vector.tensor_tensor(out=nw[:], in0=nw[:], in1=ve[:], op=ALU.mult)
+        nc.vector.tensor_scalar(out=nw[:], in0=nw[:], scalar1=-0.5, scalar2=1.5, op0=ALU.mult, op1=ALU.add)
+        nc.vector.tensor_tensor(out=rs[:], in0=rs[:], in1=nw[:], op=ALU.mult)
+        xn = const.tile([P, NT, D], F32)
+        nc.vector.tensor_tensor(out=xn[:], in0=xc[:], in1=rs[:].unsqueeze(2).to_broadcast([P, NT, D]), op=ALU.mult)
+
+        nc.vector.quantize_mx(out=w_codes[:].bitcast(FP8X4), scales=w_scl[:], in_=w_grp[:].rearrange("p w j -> p (w j)"))
+
+        out_v = out.rearrange("(p i) c -> p i c", i=NT)
+
+        for g in range(NT // QB):
+            kq = kqp.tile([P, QB * M], BF16, align_bytes=64)
+            for j in range(QB):
+                i = g * QB + j
+                ts = tsp.tile([P, NS, M], F32)
+                for k in range(NS):
+                    nc.scalar.activation(out=ts[:, k, :], in_=zb[:, k, :], func=ACT.Relu, bias=xn[:, i, k:k + 1], scale=-1.0)
+                tg = tgp.tile([P, NG, M], F32)
+                for k in range(NG):
+                    d = NS + k
+                    nc.gpsimd.tensor_scalar(out=tg[:, k, :], in0=zb[:, d, :], scalar1=BIG, scalar2=xn[:, i, d:d + 1], op0=ALU.min, op1=ALU.max)
+                tv = tvp.tile([P, M], F32)
+                for k in range(NV):
+                    d = D - NV + k
+                    prev = c_sb if k == 0 else tv
+                    nc.vector.scalar_tensor_tensor(
+                        out=tv[:], in0=zps[k // 2][:, (k % 2) * M:(k % 2 + 1) * M], scalar=xn[:, i, d:d + 1],
+                        in1=prev[:], op0=ALU.max, op1=ALU.add)
+                terms = [ts[:, k, :] for k in range(NS)] + [tg[:, k, :] for k in range(NG)] + [tv[:]]
+                acc = psa.tile([P, M], F32, tag="acc")
+                for t in range(PACK):
+                    for q, term in enumerate(terms):
+                        nc.tensor.matmul(
+                            out=acc[:, t * P:(t + 1) * P], lhsT=term[:, t * P:(t + 1) * P], rhs=ident_f[:],
+                            is_transpose=True, start=(q == 0), stop=(q == len(terms) - 1))
+                nc.scalar.activation(
+                    out=kq[:, j * M:(j + 1) * M].rearrange("p (n t) -> p n t", t=PACK),
+                    in_=acc[:].rearrange("p (t n) -> p n t", t=PACK), func=ACT.Exp, scale=-2.0)
+            codes = cqp.tile([P, QB * P], U32, align_bytes=64)
+            scl = cqp.tile([P, QB * P], U8, align_bytes=64)
+            nc.vector.quantize_mx(out=codes[:].bitcast(FP8X4), scales=scl[:], in_=kq[:])
+            o_sb = osp.tile([P, QB, POUT], F32)
+            for h in range(QB // 2):
+                ops = pso.tile([P, 2 * POUT], F32)
+                for e in range(2):
+                    j = 2 * h + e
+                    nc.tensor.matmul_mx(
+                        out=ops[:, e * POUT:(e + 1) * POUT],
+                        lhsT=codes[:, j * P:(j + 1) * P].bitcast(FP8X4), lhsT_scale=scl[:, j * P:(j + 1) * P],
+                        rhs=w_codes[:].bitcast(FP8X4), rhs_scale=w_scl[:], start=True, stop=True)
+                nc.scalar.copy(out=o_sb[:, 2 * h:2 * h + 2, :], in_=ops[:].rearrange("p (e c) -> p e c", e=2))
+            nc.sync.dma_start(out=out_v[:, g * QB:(g + 1) * QB, :], in_=o_sb[:])

@@ -24,16 +24,24 @@ NS = 5
 NG = 5
 NV = 6
 QB = 4
+BOOST = 32
+BOOST_AT = (0, 2)
+RAMP_AT = (1,)
+MANUAL = True
 
 
 def tile_tmk_t_kernel(tc, x, design_points, chol_inv, out):
     nc = tc.nc
     nsb = NS + NG
+    nsb2 = (nsb + 1) // 2
+    nvb = (NV + 1) // 2
     with ExitStack() as ctx:
+        if MANUAL:
+            ctx.enter_context(tc.manual_schedule())
         const = ctx.enter_context(tc.tile_pool(name="const", bufs=1))
         tsp = ctx.enter_context(tc.tile_pool(name="tsp", bufs=3))
         tgp = ctx.enter_context(tc.tile_pool(name="tgp", bufs=3))
-        tvp = ctx.enter_context(tc.tile_pool(name="tvp", bufs=4))
+        tvp = ctx.enter_context(tc.tile_pool(name="tvp", bufs=8))
         kqp = ctx.enter_context(tc.tile_pool(name="kqp", bufs=3))
         cqp = ctx.enter_context(tc.tile_pool(name="cqp", bufs=3))
         osp = ctx.enter_context(tc.tile_pool(name="osp", bufs=3))
@@ -41,36 +49,17 @@ def tile_tmk_t_kernel(tc, x, design_points, chol_inv, out):
         psa = ctx.enter_context(tc.psum_pool(name="psa", bufs=3))
         pso = ctx.enter_context(tc.psum_pool(name="pso", bufs=2))
 
-        x_sb = const.tile([P, NT, D], BF16)
-        nc.sync.dma_start(out=x_sb[:], in_=x.rearrange("(p i) d -> p i d", i=NT))
         z_sb = const.tile([P, PACK, D], BF16)
         nc.sync.dma_start(out=z_sb[:], in_=design_points.rearrange("(p t) d -> p t d", t=PACK))
+        x_sb = const.tile([P, NT, D], BF16)
+        nc.sync.dma_start(out=x_sb[:], in_=x.rearrange("(p i) d -> p i d", i=NT))
         w_raw = const.tile([P, PACK, POUT], BF16)
         nc.sync.dma_start(out=w_raw[:], in_=chol_inv.rearrange("(p j) w -> p j w", j=PACK))
 
-        ident_f = const.tile([P, P], F32)
-        make_identity(nc, ident_f[:])
         ident_b = const.tile([P, P], BF16)
         make_identity(nc, ident_b[:])
-
-        zb = const.tile([P, nsb, M], BF16)
-        for pair in range(nsb // 2):
-            tp = psa.tile([P, 2 * M], BF16, tag="acc")
-            for h in range(2):
-                d = 2 * pair + h
-                for t in range(PACK):
-                    c0 = h * M + t * P
-                    nc.tensor.transpose(tp[:, c0:c0 + P], z_sb[:, t, d:d + 1].to_broadcast([P, P]), ident_b[:])
-            nc.scalar.copy(out=zb[:, 2 * pair:2 * pair + 2, :], in_=tp[:].rearrange("p (h m) -> p h m", h=2))
-        zps = []
-        for b in range(NV // 2):
-            zp = psz.tile([P, 2 * M], BF16, name="zp%d" % b)
-            for h in range(2):
-                d = D - NV + 2 * b + h
-                for t in range(PACK):
-                    c0 = h * M + t * P
-                    nc.tensor.transpose(zp[:, c0:c0 + P], z_sb[:, t, d:d + 1].to_broadcast([P, P]), ident_b[:])
-            zps.append(zp)
+        ident_f = const.tile([P, P], F32)
+        make_identity(nc, ident_f[:])
 
         zf = const.tile([P, PACK, D], F32)
         nc.vector.tensor_copy(out=zf[:], in_=z_sb[:])
@@ -80,16 +69,28 @@ def tile_tmk_t_kernel(tc, x, design_points, chol_inv, out):
         nc.vector.tensor_reduce(out=s_sc[:], in_=zf[:, :, 0:NS], axis=AX.X, op=ALU.add)
         cz = const.tile([P, PACK], F32)
         nc.vector.scalar_tensor_tensor(out=cz[:], in0=s_all[:], scalar=-0.5, in1=s_sc[:], op0=ALU.mult, op1=ALU.add)
+
+        def spread(dst, d, h):
+            for t in range(PACK):
+                c0 = h * M + t * P
+                nc.tensor.transpose(dst[:, c0:c0 + P], z_sb[:, t, d:d + 1].to_broadcast([P, P]), ident_b[:])
+
+        zb = const.tile([P, 2 * nsb2, M], BF16)
+        for pair in range(nsb2):
+            tp = psa.tile([P, 2 * M], BF16, tag="acc")
+            for h in range(2):
+                spread(tp, 2 * pair + h, h)
+            nc.scalar.copy(out=zb[:, 2 * pair:2 * pair + 2, :], in_=tp[:].rearrange("p (h m) -> p h m", h=2))
+        zps = []
+        for b in range(nvb):
+            zp = psz.tile([P, 2 * M], BF16, name="zp%d" % b)
+            for h in range(2):
+                if 2 * b + h < NV:
+                    spread(zp, D - NV + 2 * b + h, h)
+            zps.append(zp)
         cp = psa.tile([P, M], F32, tag="acc")
         for t in range(PACK):
             nc.tensor.transpose(cp[:, t * P:(t + 1) * P], cz[:, t:t + 1].to_broadcast([P, P]), ident_f[:])
-        c_sb = const.tile([P, M], F32)
-        nc.vector.tensor_copy(out=c_sb[:], in_=cp[:])
-
-        w_grp = const.tile([P, POUT, PACK], BF16, align_bytes=64)
-        nc.vector.tensor_copy(out=w_grp[:], in_=w_raw[:].rearrange("p j w -> p w j"))
-        w_codes = const.tile([P, POUT], U32, align_bytes=64)
-        w_scl = const.tile([P, POUT], U8, align_bytes=64)
 
         xf = const.tile([P, NT, D], F32)
         nc.vector.tensor_copy(out=xf[:], in_=x_sb[:])
@@ -114,50 +115,120 @@ def tile_tmk_t_kernel(tc, x, design_points, chol_inv, out):
         nc.vector.tensor_tensor(out=rs[:], in0=rs[:], in1=nw[:], op=ALU.mult)
         xn = const.tile([P, NT, D], F32)
         nc.vector.tensor_tensor(out=xn[:], in0=xc[:], in1=rs[:].unsqueeze(2).to_broadcast([P, NT, D]), op=ALU.mult)
+        c_sb = const.tile([P, M], F32)
+        nc.vector.tensor_copy(out=c_sb[:], in_=cp[:])
 
-        nc.vector.quantize_mx(out=w_codes[:].bitcast(FP8X4), scales=w_scl[:], in_=w_grp[:].rearrange("p w j -> p (w j)"))
+        w_grp = const.tile([P, POUT, PACK], BF16, align_bytes=64)
+        w_codes = const.tile([P, POUT], U32, align_bytes=64)
+        w_scl = const.tile([P, POUT], U8, align_bytes=64)
 
         out_v = out.rearrange("(p i) c -> p i c", i=NT)
 
-        for g in range(NT // QB):
-            kq = kqp.tile([P, QB * M], BF16, align_bytes=64)
-            for j in range(QB):
-                i = g * QB + j
-                ts = tsp.tile([P, NS, M], F32)
-                for k in range(NS):
-                    nc.scalar.activation(out=ts[:, k, :], in_=zb[:, k, :], func=ACT.Relu, bias=xn[:, i, k:k + 1], scale=-1.0)
-                tg = tgp.tile([P, NG, M], F32)
-                for k in range(NG):
-                    d = NS + k
-                    nc.gpsimd.tensor_scalar(out=tg[:, k, :], in0=zb[:, d, :], scalar1=BIG, scalar2=xn[:, i, d:d + 1], op0=ALU.min, op1=ALU.max)
-                tv = tvp.tile([P, M], F32)
-                for k in range(NV):
-                    d = D - NV + k
+        ts_of = {}
+        tg_of = {}
+        tv_of = {}
+        acc_of = {}
+        kq_of = {}
+        cq_of = {}
+        ops_of = {}
+
+        def prod_s(i):
+            ts = tsp.tile([P, NS, M], F32, name="ts")
+            ts_of[i] = ts
+            for k in range(NS):
+                nc.scalar.activation(out=ts[:, k, :], in_=zb[:, k, :], func=ACT.Relu, bias=xn[:, i, k:k + 1], scale=-1.0)
+
+        def prod_g(i):
+            tg = tgp.tile([P, NG, M], F32, name="tg")
+            tg_of[i] = tg
+            for k in range(NG):
+                d = NS + k
+                nc.gpsimd.tensor_scalar(out=tg[:, k, :], in0=zb[:, d, :], scalar1=BIG, scalar2=xn[:, i, d:d + 1], op0=ALU.min, op1=ALU.max)
+
+        def prod_v(u):
+            for e in range(2):
+                tv_of[2 * u + e] = tvp.tile([P, M], F32, name="tv")
+            for k in range(NV):
+                d = D - NV + k
+                for e in range(2):
+                    i = 2 * u + e
+                    tv = tv_of[i]
                     prev = c_sb if k == 0 else tv
                     nc.vector.scalar_tensor_tensor(
                         out=tv[:], in0=zps[k // 2][:, (k % 2) * M:(k % 2 + 1) * M], scalar=xn[:, i, d:d + 1],
                         in1=prev[:], op0=ALU.max, op1=ALU.add)
-                terms = [ts[:, k, :] for k in range(NS)] + [tg[:, k, :] for k in range(NG)] + [tv[:]]
-                acc = psa.tile([P, M], F32, tag="acc")
-                for t in range(PACK):
-                    for q, term in enumerate(terms):
-                        nc.tensor.matmul(
-                            out=acc[:, t * P:(t + 1) * P], lhsT=term[:, t * P:(t + 1) * P], rhs=ident_f[:],
-                            is_transpose=True, start=(q == 0), stop=(q == len(terms) - 1))
-                nc.scalar.activation(
-                    out=kq[:, j * M:(j + 1) * M].rearrange("p (n t) -> p n t", t=PACK),
-                    in_=acc[:].rearrange("p (t n) -> p n t", t=PACK), func=ACT.Exp, scale=-2.0)
-            codes = cqp.tile([P, QB * P], U32, align_bytes=64)
-            scl = cqp.tile([P, QB * P], U8, align_bytes=64)
-            nc.vector.quantize_mx(out=codes[:].bitcast(FP8X4), scales=scl[:], in_=kq[:])
-            o_sb = osp.tile([P, QB, POUT], F32)
+
+        def pe_t(i):
+            ts = ts_of[i]
+            tg = tg_of[i]
+            terms = [ts[:, k, :] for k in range(NS)] + [tg[:, k, :] for k in range(NG)] + [tv_of[i][:]]
+            acc = psa.tile([P, M], F32, tag="acc", name="acc")
+            acc_of[i] = acc
+            if i in RAMP_AT:
+                for r in range(2):
+                    nc.tensor.matmul(out=acc[:, 0:P], lhsT=ident_f[:], rhs=ident_f[:], start=True, stop=True)
+            for t in range(PACK):
+                if BOOST > 0 and t in BOOST_AT:
+                    nc.tensor.matmul(out=acc[:, t * P:t * P + BOOST], lhsT=ident_f[:], rhs=ident_f[:, 0:BOOST], start=True, stop=True)
+                for q, term in enumerate(terms):
+                    nc.tensor.matmul(
+                        out=acc[:, t * P:(t + 1) * P], lhsT=term[:, t * P:(t + 1) * P], rhs=ident_f[:],
+                        is_transpose=True, start=(q == 0), stop=(q == len(terms) - 1))
+
+        def expo(i):
+            g = i // QB
+            j = i % QB
+            if j == 0:
+                kq_of[g] = kqp.tile([P, QB * M], BF16, align_bytes=64, name="kq")
+            kq = kq_of[g]
+            nc.scalar.activation(
+                out=kq[:, j * M:(j + 1) * M].rearrange("p (n t) -> p n t", t=PACK),
+                in_=acc_of[i][:].rearrange("p (t n) -> p n t", t=PACK), func=ACT.Exp, scale=-2.0)
+
+        def quant(g):
+            codes = cqp.tile([P, QB * P], U32, align_bytes=64, name="codes")
+            scl = cqp.tile([P, QB * P], U8, align_bytes=64, name="scl")
+            cq_of[g] = (codes, scl)
+            nc.vector.quantize_mx(out=codes[:].bitcast(FP8X4), scales=scl[:], in_=kq_of[g][:])
+
+        def mx(g):
+            codes, scl = cq_of[g]
+            banks = []
             for h in range(QB // 2):
-                ops = pso.tile([P, 2 * POUT], F32)
+                ops = pso.tile([P, 2 * POUT], F32, name="ops")
+                banks.append(ops)
                 for e in range(2):
                     j = 2 * h + e
                     nc.tensor.matmul_mx(
                         out=ops[:, e * POUT:(e + 1) * POUT],
                         lhsT=codes[:, j * P:(j + 1) * P].bitcast(FP8X4), lhsT_scale=scl[:, j * P:(j + 1) * P],
                         rhs=w_codes[:].bitcast(FP8X4), rhs_scale=w_scl[:], start=True, stop=True)
-                nc.scalar.copy(out=o_sb[:, 2 * h:2 * h + 2, :], in_=ops[:].rearrange("p (e c) -> p e c", e=2))
+            ops_of[g] = banks
+
+        def evac(g):
+            o_sb = osp.tile([P, QB, POUT], F32, name="o_sb")
+            for h in range(QB // 2):
+                src = ops_of[g][h][:].rearrange("p (e c) -> p e c", e=2)
+                nc.scalar.copy(out=o_sb[:, 2 * h:2 * h + 2, :], in_=src)
             nc.sync.dma_start(out=out_v[:, g * QB:(g + 1) * QB, :], in_=o_sb[:])
+
+        for s in range(NT + 6):
+            if s % 2 == 0 and s < NT:
+                prod_v(s // 2)
+            if s == 0:
+                nc.vector.tensor_copy(out=w_grp[:], in_=w_raw[:].rearrange("p j w -> p w j"))
+            if s == 2:
+                nc.vector.quantize_mx(out=w_codes[:].bitcast(FP8X4), scales=w_scl[:], in_=w_grp[:].rearrange("p w j -> p (w j)"))
+            if s < NT:
+                prod_s(s)
+                prod_g(s)
+            if s >= QB + 5 and (s - 5) % QB == 0:
+                evac((s - 5) // QB - 1)
+            if 0 <= s - 1 < NT:
+                pe_t(s - 1)
+            if s >= QB + 3 and (s - 3) % QB == 0:
+                mx((s - 3) // QB - 1)
+            if 0 <= s - 2 < NT:
+                expo(s - 2)
+            if s >= QB + 2 and (s - 2) % QB == 0:
+                quant((s - 2) // QB - 1)

@@ -15,6 +15,7 @@ AX = mybir.AxisListType
 N, M, POUT, D = 8192, 512, 256, 16
 P = 128
 NT = N // P
+NU = NT // 2
 PACK = 4
 LN_EPS = 1e-5
 BIG = 3.0e38
@@ -23,31 +24,25 @@ FLOPS = 2 * N * M * POUT
 NS = 5
 NG = 5
 NV = 6
-QB = 4
-BOOST = 32
-BOOST_AT = (0, 2)
-RAMP_AT = (1,)
-MANUAL = True
+INTER = True
 
 
 def tile_tmk_t_kernel(tc, x, design_points, chol_inv, out):
     nc = tc.nc
-    nsb = NS + NG
-    nsb2 = (nsb + 1) // 2
+    nsb2 = (NS + NG + 1) // 2
     nvb = (NV + 1) // 2
     with ExitStack() as ctx:
-        if MANUAL:
-            ctx.enter_context(tc.manual_schedule())
+        ctx.enter_context(tc.manual_schedule())
         const = ctx.enter_context(tc.tile_pool(name="const", bufs=1))
-        tsp = ctx.enter_context(tc.tile_pool(name="tsp", bufs=3))
-        tgp = ctx.enter_context(tc.tile_pool(name="tgp", bufs=3))
+        tsp = ctx.enter_context(tc.tile_pool(name="tsp", bufs=5))
+        tgp = ctx.enter_context(tc.tile_pool(name="tgp", bufs=5))
         tvp = ctx.enter_context(tc.tile_pool(name="tvp", bufs=8))
         kqp = ctx.enter_context(tc.tile_pool(name="kqp", bufs=3))
         cqp = ctx.enter_context(tc.tile_pool(name="cqp", bufs=3))
         osp = ctx.enter_context(tc.tile_pool(name="osp", bufs=3))
         psz = ctx.enter_context(tc.psum_pool(name="psz", bufs=1))
-        psa = ctx.enter_context(tc.psum_pool(name="psa", bufs=3))
-        pso = ctx.enter_context(tc.psum_pool(name="pso", bufs=2))
+        psa = ctx.enter_context(tc.psum_pool(name="psa", bufs=4))
+        pso = ctx.enter_context(tc.psum_pool(name="pso", bufs=1))
 
         z_sb = const.tile([P, PACK, D], BF16)
         nc.sync.dma_start(out=z_sb[:], in_=design_points.rearrange("(p t) d -> p t d", t=PACK))
@@ -158,77 +153,86 @@ def tile_tmk_t_kernel(tc, x, design_points, chol_inv, out):
                         out=tv[:], in0=zps[k // 2][:, (k % 2) * M:(k % 2 + 1) * M], scalar=xn[:, i, d:d + 1],
                         in1=prev[:], op0=ALU.max, op1=ALU.add)
 
-        def pe_t(i):
-            ts = ts_of[i]
-            tg = tg_of[i]
-            terms = [ts[:, k, :] for k in range(NS)] + [tg[:, k, :] for k in range(NG)] + [tv_of[i][:]]
-            acc = psa.tile([P, M], F32, tag="acc", name="acc")
-            acc_of[i] = acc
-            if i in RAMP_AT:
-                for r in range(2):
-                    nc.tensor.matmul(out=acc[:, 0:P], lhsT=ident_f[:], rhs=ident_f[:], start=True, stop=True)
-            for t in range(PACK):
-                if BOOST > 0 and t in BOOST_AT:
-                    nc.tensor.matmul(out=acc[:, t * P:t * P + BOOST], lhsT=ident_f[:], rhs=ident_f[:, 0:BOOST], start=True, stop=True)
-                for q, term in enumerate(terms):
-                    nc.tensor.matmul(
-                        out=acc[:, t * P:(t + 1) * P], lhsT=term[:, t * P:(t + 1) * P], rhs=ident_f[:],
-                        is_transpose=True, start=(q == 0), stop=(q == len(terms) - 1))
+        def terms_of(i):
+            return [ts_of[i][:, k, :] for k in range(NS)] + [tg_of[i][:, k, :] for k in range(NG)] + [tv_of[i][:]]
+
+        def add_term(i, t, q, terms):
+            nc.tensor.matmul(
+                out=acc_of[i][:, t * P:(t + 1) * P], lhsT=terms[q][:, t * P:(t + 1) * P], rhs=ident_f[:],
+                is_transpose=True, start=(q == 0), stop=(q == len(terms) - 1))
+
+        def pe_pair(u):
+            both = (2 * u, 2 * u + 1)
+            terms = {}
+            for i in both:
+                acc_of[i] = psa.tile([P, M], F32, tag="acc", name="acc")
+                terms[i] = terms_of(i)
+            nq = NS + NG + 1
+            if INTER:
+                for t in range(PACK):
+                    for q in range(nq):
+                        for i in both:
+                            add_term(i, t, q, terms[i])
+            else:
+                for i in both:
+                    for t in range(PACK):
+                        for q in range(nq):
+                            add_term(i, t, q, terms[i])
 
         def expo(i):
-            g = i // QB
-            j = i % QB
+            g = i // 2
+            j = i % 2
             if j == 0:
-                kq_of[g] = kqp.tile([P, QB * M], BF16, align_bytes=64, name="kq")
+                kq_of[g] = kqp.tile([P, 2 * M], BF16, align_bytes=64, name="kq")
             kq = kq_of[g]
             nc.scalar.activation(
                 out=kq[:, j * M:(j + 1) * M].rearrange("p (n t) -> p n t", t=PACK),
                 in_=acc_of[i][:].rearrange("p (t n) -> p n t", t=PACK), func=ACT.Exp, scale=-2.0)
 
         def quant(g):
-            codes = cqp.tile([P, QB * P], U32, align_bytes=64, name="codes")
-            scl = cqp.tile([P, QB * P], U8, align_bytes=64, name="scl")
+            codes = cqp.tile([P, 2 * P], U32, align_bytes=64, name="codes")
+            scl = cqp.tile([P, 2 * P], U8, align_bytes=64, name="scl")
             cq_of[g] = (codes, scl)
             nc.vector.quantize_mx(out=codes[:].bitcast(FP8X4), scales=scl[:], in_=kq_of[g][:])
 
         def mx(g):
             codes, scl = cq_of[g]
-            banks = []
-            for h in range(QB // 2):
-                ops = pso.tile([P, 2 * POUT], F32, name="ops")
-                banks.append(ops)
-                for e in range(2):
-                    j = 2 * h + e
-                    nc.tensor.matmul_mx(
-                        out=ops[:, e * POUT:(e + 1) * POUT],
-                        lhsT=codes[:, j * P:(j + 1) * P].bitcast(FP8X4), lhsT_scale=scl[:, j * P:(j + 1) * P],
-                        rhs=w_codes[:].bitcast(FP8X4), rhs_scale=w_scl[:], start=True, stop=True)
-            ops_of[g] = banks
+            ops = pso.tile([P, 2 * POUT], F32, name="ops")
+            for e in range(2):
+                nc.tensor.matmul_mx(
+                    out=ops[:, e * POUT:(e + 1) * POUT],
+                    lhsT=codes[:, e * P:(e + 1) * P].bitcast(FP8X4), lhsT_scale=scl[:, e * P:(e + 1) * P],
+                    rhs=w_codes[:].bitcast(FP8X4), rhs_scale=w_scl[:], start=True, stop=True)
+            ops_of[g] = ops
 
         def evac(g):
-            o_sb = osp.tile([P, QB, POUT], F32, name="o_sb")
-            for h in range(QB // 2):
-                src = ops_of[g][h][:].rearrange("p (e c) -> p e c", e=2)
-                nc.scalar.copy(out=o_sb[:, 2 * h:2 * h + 2, :], in_=src)
-            nc.sync.dma_start(out=out_v[:, g * QB:(g + 1) * QB, :], in_=o_sb[:])
+            o_sb = osp.tile([P, 2, POUT], F32, name="o_sb")
+            src = ops_of[g][:].rearrange("p (e c) -> p e c", e=2)
+            nc.scalar.copy(out=o_sb[:], in_=src)
+            nc.sync.dma_start(out=out_v[:, 2 * g:2 * g + 2, :], in_=o_sb[:])
 
-        for s in range(NT + 6):
-            if s % 2 == 0 and s < NT:
-                prod_v(s // 2)
-            if s == 0:
+        for u in range(NU + 5):
+            if 0 <= u - 3 < NU:
+                quant(u - 3)
+            if u < NU:
+                prod_v(u)
+            if u == 0:
                 nc.vector.tensor_copy(out=w_grp[:], in_=w_raw[:].rearrange("p j w -> p w j"))
-            if s == 2:
+            if u == 1:
                 nc.vector.quantize_mx(out=w_codes[:].bitcast(FP8X4), scales=w_scl[:], in_=w_grp[:].rearrange("p w j -> p (w j)"))
-            if s < NT:
-                prod_s(s)
-                prod_g(s)
-            if s >= QB + 5 and (s - 5) % QB == 0:
-                evac((s - 5) // QB - 1)
-            if 0 <= s - 1 < NT:
-                pe_t(s - 1)
-            if s >= QB + 3 and (s - 3) % QB == 0:
-                mx((s - 3) // QB - 1)
-            if 0 <= s - 2 < NT:
-                expo(s - 2)
-            if s >= QB + 2 and (s - 2) % QB == 0:
-                quant((s - 2) // QB - 1)
+            if u < NU:
+                prod_s(2 * u)
+                prod_g(2 * u)
+            if 0 <= u - 4 < NU:
+                evac(u - 4)
+            if 0 <= u - 2 < NU:
+                expo(2 * (u - 2))
+            if u < NU:
+                prod_s(2 * u + 1)
+                prod_g(2 * u + 1)
+            if 0 <= u - 2 < NU:
+                expo(2 * (u - 2) + 1)
+            if 0 <= u - 1 < NU:
+                pe_pair(u - 1)
+            if 0 <= u - 3 < NU:
+                mx(u - 3)

@@ -15,34 +15,38 @@ AX = mybir.AxisListType
 N, M, POUT, D = 8192, 512, 256, 16
 P = 128
 NT = N // P
-NU = NT // 2
 PACK = 4
 LN_EPS = 1e-5
 BIG = 3.0e38
 FLOPS = 2 * N * M * POUT
 
 NS = 5
-NG = 5
-NV = 6
-INTER = True
+NG = 4
+NVS = 1
+NVP = 6
+EVN = 2
+REC = 4
+RECP = 4
+LAG = 4
+assert NS + NG + NVS + NVP == D
 
 
 def tile_tmk_t_kernel(tc, x, design_points, chol_inv, out):
     nc = tc.nc
-    nsb2 = (NS + NG + 1) // 2
-    nvb = (NV + 1) // 2
+    nsb2 = (NS + NG + NVS + 1) // 2
+    nvb = (NVP + 1) // 2
     with ExitStack() as ctx:
         ctx.enter_context(tc.manual_schedule())
         const = ctx.enter_context(tc.tile_pool(name="const", bufs=1))
-        tsp = ctx.enter_context(tc.tile_pool(name="tsp", bufs=5))
-        tgp = ctx.enter_context(tc.tile_pool(name="tgp", bufs=5))
+        tsp = ctx.enter_context(tc.tile_pool(name="tsp", bufs=4))
+        tgp = ctx.enter_context(tc.tile_pool(name="tgp", bufs=4))
         tvp = ctx.enter_context(tc.tile_pool(name="tvp", bufs=8))
-        kqp = ctx.enter_context(tc.tile_pool(name="kqp", bufs=3))
-        cqp = ctx.enter_context(tc.tile_pool(name="cqp", bufs=3))
+        kqp = ctx.enter_context(tc.tile_pool(name="kqp", bufs=4))
+        cqp = ctx.enter_context(tc.tile_pool(name="cqp", bufs=10))
         osp = ctx.enter_context(tc.tile_pool(name="osp", bufs=3))
         psz = ctx.enter_context(tc.psum_pool(name="psz", bufs=1))
-        psa = ctx.enter_context(tc.psum_pool(name="psa", bufs=4))
-        pso = ctx.enter_context(tc.psum_pool(name="pso", bufs=1))
+        psa = ctx.enter_context(tc.psum_pool(name="psa", bufs=3))
+        pso = ctx.enter_context(tc.psum_pool(name="pso", bufs=2))
 
         z_sb = const.tile([P, PACK, D], BF16)
         nc.sync.dma_start(out=z_sb[:], in_=design_points.rearrange("(p t) d -> p t d", t=PACK))
@@ -65,6 +69,11 @@ def tile_tmk_t_kernel(tc, x, design_points, chol_inv, out):
         cz = const.tile([P, PACK], F32)
         nc.vector.scalar_tensor_tensor(out=cz[:], in0=s_all[:], scalar=-0.5, in1=s_sc[:], op0=ALU.mult, op1=ALU.add)
 
+        w_grp = const.tile([P, POUT, PACK], BF16, align_bytes=64)
+        w_codes = const.tile([P, POUT], U32, align_bytes=64)
+        w_scl = const.tile([P, POUT], U8, align_bytes=64)
+        nc.scalar.copy(out=w_grp[:], in_=w_raw[:].rearrange("p j w -> p w j"))
+
         def spread(dst, d, h):
             for t in range(PACK):
                 c0 = h * M + t * P
@@ -80,8 +89,8 @@ def tile_tmk_t_kernel(tc, x, design_points, chol_inv, out):
         for b in range(nvb):
             zp = psz.tile([P, 2 * M], BF16, name="zp%d" % b)
             for h in range(2):
-                if 2 * b + h < NV:
-                    spread(zp, D - NV + 2 * b + h, h)
+                if 2 * b + h < NVP:
+                    spread(zp, D - NVP + 2 * b + h, h)
             zps.append(zp)
         cp = psa.tile([P, M], F32, tag="acc")
         for t in range(PACK):
@@ -101,6 +110,7 @@ def tile_tmk_t_kernel(tc, x, design_points, chol_inv, out):
         nc.vector.tensor_scalar(out=ve[:], in0=ve[:], scalar1=1.0 / D, scalar2=LN_EPS, op0=ALU.mult, op1=ALU.add)
         sd = const.tile([P, NT], F32)
         nc.scalar.activation(out=sd[:], in_=ve[:], func=ACT.Sqrt)
+        nc.vector.quantize_mx(out=w_codes[:].bitcast(FP8X4), scales=w_scl[:], in_=w_grp[:].rearrange("p w j -> p (w j)"))
         rs = const.tile([P, NT], F32)
         nc.vector.reciprocal(out=rs[:], in_=sd[:])
         nw = const.tile([P, NT], F32)
@@ -112,10 +122,6 @@ def tile_tmk_t_kernel(tc, x, design_points, chol_inv, out):
         nc.vector.tensor_tensor(out=xn[:], in0=xc[:], in1=rs[:].unsqueeze(2).to_broadcast([P, NT, D]), op=ALU.mult)
         c_sb = const.tile([P, M], F32)
         nc.vector.tensor_copy(out=c_sb[:], in_=cp[:])
-
-        w_grp = const.tile([P, POUT, PACK], BF16, align_bytes=64)
-        w_codes = const.tile([P, POUT], U32, align_bytes=64)
-        w_scl = const.tile([P, POUT], U8, align_bytes=64)
 
         out_v = out.rearrange("(p i) c -> p i c", i=NT)
 
@@ -143,96 +149,83 @@ def tile_tmk_t_kernel(tc, x, design_points, chol_inv, out):
         def prod_v(u):
             for e in range(2):
                 tv_of[2 * u + e] = tvp.tile([P, M], F32, name="tv")
-            for k in range(NV):
-                d = D - NV + k
+            for k in range(NVS + NVP):
+                d = NS + NG + k
+                if k < NVS:
+                    table = zb[:, d, :]
+                else:
+                    kp = k - NVS
+                    table = zps[kp // 2][:, (kp % 2) * M:(kp % 2 + 1) * M]
                 for e in range(2):
                     i = 2 * u + e
                     tv = tv_of[i]
                     prev = c_sb if k == 0 else tv
                     nc.vector.scalar_tensor_tensor(
-                        out=tv[:], in0=zps[k // 2][:, (k % 2) * M:(k % 2 + 1) * M], scalar=xn[:, i, d:d + 1],
-                        in1=prev[:], op0=ALU.max, op1=ALU.add)
+                        out=tv[:], in0=table, scalar=xn[:, i, d:d + 1], in1=prev[:], op0=ALU.max, op1=ALU.add)
 
-        def terms_of(i):
-            return [ts_of[i][:, k, :] for k in range(NS)] + [tg_of[i][:, k, :] for k in range(NG)] + [tv_of[i][:]]
-
-        def add_term(i, t, q, terms):
-            nc.tensor.matmul(
-                out=acc_of[i][:, t * P:(t + 1) * P], lhsT=terms[q][:, t * P:(t + 1) * P], rhs=ident_f[:],
-                is_transpose=True, start=(q == 0), stop=(q == len(terms) - 1))
-
-        def pe_pair(u):
-            both = (2 * u, 2 * u + 1)
-            terms = {}
-            for i in both:
-                acc_of[i] = psa.tile([P, M], F32, tag="acc", name="acc")
-                terms[i] = terms_of(i)
-            nq = NS + NG + 1
-            if INTER:
-                for t in range(PACK):
-                    for q in range(nq):
-                        for i in both:
-                            add_term(i, t, q, terms[i])
+        def mx_pass(j):
+            g = max(j, 0) // 2
+            e = max(j, 0) % 2
+            if g not in ops_of:
+                ops_of[g] = pso.tile([P, 2 * POUT], F32, name="ops")
+            if j < 0:
+                lhs, lhs_s = w_codes[:, 0:P], w_scl[:, 0:P]
             else:
-                for i in both:
-                    for t in range(PACK):
-                        for q in range(nq):
-                            add_term(i, t, q, terms[i])
+                lhs, lhs_s = cq_of[j][0][:], cq_of[j][1][:]
+            nc.tensor.matmul_mx(
+                out=ops_of[g][:, e * POUT:(e + 1) * POUT], lhsT=lhs.bitcast(FP8X4), lhsT_scale=lhs_s,
+                rhs=w_codes[:].bitcast(FP8X4), rhs_scale=w_scl[:], start=True, stop=True)
+
+        def pe_tile(i):
+            terms = [ts_of[i][:, k, :] for k in range(NS)] + [tg_of[i][:, k, :] for k in range(NG)] + [tv_of[i][:]]
+            acc = psa.tile([P, M], F32, tag="acc", name="acc")
+            acc_of[i] = acc
+            for t in range(PACK):
+                for q, term in enumerate(terms):
+                    nc.tensor.matmul(
+                        out=acc[:, t * P:(t + 1) * P], lhsT=term[:, t * P:(t + 1) * P], rhs=ident_f[:],
+                        is_transpose=True, start=(q == 0), stop=(q == len(terms) - 1))
+                if t % 2 == 1:
+                    n = EVN
+                    if t == 1 and i % RECP == 0:
+                        n = EVN + REC
+                    for r in range(n):
+                        mx_pass(i - LAG)
 
         def expo(i):
-            g = i // 2
-            j = i % 2
-            if j == 0:
-                kq_of[g] = kqp.tile([P, 2 * M], BF16, align_bytes=64, name="kq")
-            kq = kq_of[g]
+            kq = kqp.tile([P, M], BF16, align_bytes=64, name="kq")
+            kq_of[i] = kq
             nc.scalar.activation(
-                out=kq[:, j * M:(j + 1) * M].rearrange("p (n t) -> p n t", t=PACK),
+                out=kq[:].rearrange("p (n t) -> p n t", t=PACK),
                 in_=acc_of[i][:].rearrange("p (t n) -> p n t", t=PACK), func=ACT.Exp, scale=-2.0)
 
-        def quant(g):
-            codes = cqp.tile([P, 2 * P], U32, align_bytes=64, name="codes")
-            scl = cqp.tile([P, 2 * P], U8, align_bytes=64, name="scl")
-            cq_of[g] = (codes, scl)
-            nc.vector.quantize_mx(out=codes[:].bitcast(FP8X4), scales=scl[:], in_=kq_of[g][:])
-
-        def mx(g):
-            codes, scl = cq_of[g]
-            ops = pso.tile([P, 2 * POUT], F32, name="ops")
-            for e in range(2):
-                nc.tensor.matmul_mx(
-                    out=ops[:, e * POUT:(e + 1) * POUT],
-                    lhsT=codes[:, e * P:(e + 1) * P].bitcast(FP8X4), lhsT_scale=scl[:, e * P:(e + 1) * P],
-                    rhs=w_codes[:].bitcast(FP8X4), rhs_scale=w_scl[:], start=True, stop=True)
-            ops_of[g] = ops
+        def quant(i):
+            codes = cqp.tile([P, P], U32, align_bytes=64, name="codes")
+            scl = cqp.tile([P, P], U8, align_bytes=64, name="scl")
+            cq_of[i] = (codes, scl)
+            nc.vector.quantize_mx(out=codes[:].bitcast(FP8X4), scales=scl[:], in_=kq_of[i][:])
 
         def evac(g):
             o_sb = osp.tile([P, 2, POUT], F32, name="o_sb")
-            src = ops_of[g][:].rearrange("p (e c) -> p e c", e=2)
-            nc.scalar.copy(out=o_sb[:], in_=src)
+            nc.scalar.copy(out=o_sb[:], in_=ops_of[g][:].rearrange("p (e c) -> p e c", e=2))
             nc.sync.dma_start(out=out_v[:, 2 * g:2 * g + 2, :], in_=o_sb[:])
 
-        for u in range(NU + 5):
-            if 0 <= u - 3 < NU:
-                quant(u - 3)
-            if u < NU:
-                prod_v(u)
-            if u == 0:
-                nc.vector.tensor_copy(out=w_grp[:], in_=w_raw[:].rearrange("p j w -> p w j"))
-            if u == 1:
-                nc.vector.quantize_mx(out=w_codes[:].bitcast(FP8X4), scales=w_scl[:], in_=w_grp[:].rearrange("p w j -> p (w j)"))
-            if u < NU:
-                prod_s(2 * u)
-                prod_g(2 * u)
-            if 0 <= u - 4 < NU:
-                evac(u - 4)
-            if 0 <= u - 2 < NU:
-                expo(2 * (u - 2))
-            if u < NU:
-                prod_s(2 * u + 1)
-                prod_g(2 * u + 1)
-            if 0 <= u - 2 < NU:
-                expo(2 * (u - 2) + 1)
-            if 0 <= u - 1 < NU:
-                pe_pair(u - 1)
-            if 0 <= u - 3 < NU:
-                mx(u - 3)
+        for s in range(NT + LAG + 4):
+            if s % 2 == 0:
+                for i in (s - 4, s - 3):
+                    if 0 <= i < NT:
+                        quant(i)
+                if s < NT:
+                    prod_v(s // 2)
+            if s < NT:
+                prod_s(s)
+                prod_g(s)
+            ge = s - LAG - 3
+            if ge >= 0 and ge % 2 == 0 and ge // 2 < NT // 2:
+                evac(ge // 2)
+            if 0 <= s - 2 < NT:
+                expo(s - 2)
+            if 0 <= s - 1 < NT:
+                pe_tile(s - 1)
+            elif NT <= s - 1 < NT + LAG:
+                mx_pass(s - 1 - LAG)

@@ -20,8 +20,8 @@ LN_EPS = 1e-5
 BIG = 3.0e38
 FLOPS = 2 * N * M * POUT
 
-NS = 5
-NG = 4
+NS = 6
+NG = 3
 NVS = 1
 NVP = 6
 EVN = 2

@@ -20,10 +20,10 @@ LN_EPS = 1e-5
 BIG = 3.0e38
 FLOPS = 2 * N * M * POUT
 
-NS = 6
+NS = 5
 NG = 3
-NVS = 1
-NVP = 6
+NVS = 0
+NVP = 8
 EVN = 2
 REC = 4
 RECP = 4
@@ -45,7 +45,7 @@ def tile_tmk_t_kernel(tc, x, design_points, chol_inv, out):
         cqp = ctx.enter_context(tc.tile_pool(name="cqp", bufs=10))
         osp = ctx.enter_context(tc.tile_pool(name="osp", bufs=3))
         psz = ctx.enter_context(tc.psum_pool(name="psz", bufs=1))
-        psa = ctx.enter_context(tc.psum_pool(name="psa", bufs=3))
+        psa = ctx.enter_context(tc.psum_pool(name="psa", bufs=2))
         pso = ctx.enter_context(tc.psum_pool(name="pso", bufs=2))
 
         z_sb = const.tile([P, PACK, D], BF16)

@@ -20,8 +20,8 @@ LN_EPS = 1e-5
 BIG = 3.0e38
 FLOPS = 2 * N * M * POUT
 
-NS = 5
-NG = 3
+NS = 7
+NG = 1
 NVS = 0
 NVP = 8
 EVN = 2

@@ -22,30 +22,32 @@ FLOPS = 2 * N * M * POUT
 
 NS = 7
 NG = 1
-NVS = 0
-NVP = 8
+NADD = 0
+NV = 8
 EVN = 2
 REC = 4
 RECP = 4
-LAG = 4
-assert NS + NG + NVS + NVP == D
+QG = 4
+LAG = 6
+assert NS + NG + NV == D
+assert 2 * NADD <= NS
 
 
 def tile_tmk_t_kernel(tc, x, design_points, chol_inv, out):
     nc = tc.nc
-    nsb2 = (NS + NG + NVS + 1) // 2
-    nvb = (NVP + 1) // 2
+    nsb2 = (NS + NG + 1) // 2
+    nvb = (NV + 1) // 2
     with ExitStack() as ctx:
         ctx.enter_context(tc.manual_schedule())
         const = ctx.enter_context(tc.tile_pool(name="const", bufs=1))
         tsp = ctx.enter_context(tc.tile_pool(name="tsp", bufs=4))
         tgp = ctx.enter_context(tc.tile_pool(name="tgp", bufs=4))
-        tvp = ctx.enter_context(tc.tile_pool(name="tvp", bufs=8))
-        kqp = ctx.enter_context(tc.tile_pool(name="kqp", bufs=4))
-        cqp = ctx.enter_context(tc.tile_pool(name="cqp", bufs=10))
+        tvp = ctx.enter_context(tc.tile_pool(name="tvp", bufs=4))
+        kqp = ctx.enter_context(tc.tile_pool(name="kqp", bufs=3))
+        cqp = ctx.enter_context(tc.tile_pool(name="cqp", bufs=3))
         osp = ctx.enter_context(tc.tile_pool(name="osp", bufs=3))
         psz = ctx.enter_context(tc.psum_pool(name="psz", bufs=1))
-        psa = ctx.enter_context(tc.psum_pool(name="psa", bufs=2))
+        psa = ctx.enter_context(tc.psum_pool(name="psa", bufs=8 - 2 - nvb))
         pso = ctx.enter_context(tc.psum_pool(name="pso", bufs=2))
 
         z_sb = const.tile([P, PACK, D], BF16)
@@ -89,8 +91,8 @@ def tile_tmk_t_kernel(tc, x, design_points, chol_inv, out):
         for b in range(nvb):
             zp = psz.tile([P, 2 * M], BF16, name="zp%d" % b)
             for h in range(2):
-                if 2 * b + h < NVP:
-                    spread(zp, D - NVP + 2 * b + h, h)
+                if 2 * b + h < NV:
+                    spread(zp, D - NV + 2 * b + h, h)
             zps.append(zp)
         cp = psa.tile([P, M], F32, tag="acc")
         for t in range(PACK):
@@ -140,28 +142,26 @@ def tile_tmk_t_kernel(tc, x, design_points, chol_inv, out):
                 nc.scalar.activation(out=ts[:, k, :], in_=zb[:, k, :], func=ACT.Relu, bias=xn[:, i, k:k + 1], scale=-1.0)
 
         def prod_g(i):
-            tg = tgp.tile([P, NG, M], F32, name="tg")
+            tg = tgp.tile([P, max(NG, 1), M], F32, name="tg")
             tg_of[i] = tg
             for k in range(NG):
                 d = NS + k
                 nc.gpsimd.tensor_scalar(out=tg[:, k, :], in0=zb[:, d, :], scalar1=BIG, scalar2=xn[:, i, d:d + 1], op0=ALU.min, op1=ALU.max)
 
-        def prod_v(u):
-            for e in range(2):
-                tv_of[2 * u + e] = tvp.tile([P, M], F32, name="tv")
-            for k in range(NVS + NVP):
-                d = NS + NG + k
-                if k < NVS:
-                    table = zb[:, d, :]
-                else:
-                    kp = k - NVS
-                    table = zps[kp // 2][:, (kp % 2) * M:(kp % 2 + 1) * M]
-                for e in range(2):
-                    i = 2 * u + e
-                    tv = tv_of[i]
-                    prev = c_sb if k == 0 else tv
-                    nc.vector.scalar_tensor_tensor(
-                        out=tv[:], in0=table, scalar=xn[:, i, d:d + 1], in1=prev[:], op0=ALU.max, op1=ALU.add)
+        def add_g(i):
+            ts = ts_of[i]
+            for a in range(NADD):
+                nc.gpsimd.tensor_tensor(out=ts[:, 2 * a, :], in0=ts[:, 2 * a, :], in1=ts[:, 2 * a + 1, :], op=ALU.add)
+
+        def chain_v(i, k):
+            if k == 0:
+                tv_of[i] = tvp.tile([P, M], F32, name="tv")
+            tv = tv_of[i]
+            d = NS + NG + k
+            table = zps[k // 2][:, (k % 2) * M:(k % 2 + 1) * M]
+            prev = c_sb if k == 0 else tv
+            nc.vector.scalar_tensor_tensor(
+                out=tv[:], in0=table, scalar=xn[:, i, d:d + 1], in1=prev[:], op0=ALU.max, op1=ALU.add)
 
         def mx_pass(j):
             g = max(j, 0) // 2
@@ -171,13 +171,19 @@ def tile_tmk_t_kernel(tc, x, design_points, chol_inv, out):
             if j < 0:
                 lhs, lhs_s = w_codes[:, 0:P], w_scl[:, 0:P]
             else:
-                lhs, lhs_s = cq_of[j][0][:], cq_of[j][1][:]
+                codes, scl = cq_of[j // QG]
+                r = j % QG
+                lhs, lhs_s = codes[:, r * P:(r + 1) * P], scl[:, r * P:(r + 1) * P]
             nc.tensor.matmul_mx(
                 out=ops_of[g][:, e * POUT:(e + 1) * POUT], lhsT=lhs.bitcast(FP8X4), lhsT_scale=lhs_s,
                 rhs=w_codes[:].bitcast(FP8X4), rhs_scale=w_scl[:], start=True, stop=True)
 
         def pe_tile(i):
-            terms = [ts_of[i][:, k, :] for k in range(NS)] + [tg_of[i][:, k, :] for k in range(NG)] + [tv_of[i][:]]
+            ts = ts_of[i]
+            terms = [tv_of[i][:]]
+            terms += [ts[:, 2 * a, :] for a in range(NADD)]
+            terms += [tg_of[i][:, k, :] for k in range(NG)]
+            terms += [ts[:, k, :] for k in range(2 * NADD, NS)]
             acc = psa.tile([P, M], F32, tag="acc", name="acc")
             acc_of[i] = acc
             for t in range(PACK):
@@ -193,39 +199,45 @@ def tile_tmk_t_kernel(tc, x, design_points, chol_inv, out):
                         mx_pass(i - LAG)
 
         def expo(i):
-            kq = kqp.tile([P, M], BF16, align_bytes=64, name="kq")
-            kq_of[i] = kq
+            if i % QG == 0:
+                kq_of[i // QG] = kqp.tile([P, QG, M], BF16, align_bytes=64, name="kq")
+            kq = kq_of[i // QG]
             nc.scalar.activation(
-                out=kq[:].rearrange("p (n t) -> p n t", t=PACK),
+                out=kq[:, i % QG, :].rearrange("p (n t) -> p n t", t=PACK),
                 in_=acc_of[i][:].rearrange("p (t n) -> p n t", t=PACK), func=ACT.Exp, scale=-2.0)
 
-        def quant(i):
-            codes = cqp.tile([P, P], U32, align_bytes=64, name="codes")
-            scl = cqp.tile([P, P], U8, align_bytes=64, name="scl")
-            cq_of[i] = (codes, scl)
-            nc.vector.quantize_mx(out=codes[:].bitcast(FP8X4), scales=scl[:], in_=kq_of[i][:])
+        def quant(g):
+            codes = cqp.tile([P, QG * P], U32, align_bytes=64, name="codes")
+            scl = cqp.tile([P, QG * P], U8, align_bytes=64, name="scl")
+            cq_of[g] = (codes, scl)
+            nc.vector.quantize_mx(out=codes[:].bitcast(FP8X4), scales=scl[:], in_=kq_of[g][:].rearrange("p g m -> p (g m)"))
 
         def evac(g):
             o_sb = osp.tile([P, 2, POUT], F32, name="o_sb")
             nc.scalar.copy(out=o_sb[:], in_=ops_of[g][:].rearrange("p (e c) -> p e c", e=2))
             nc.sync.dma_start(out=out_v[:, 2 * g:2 * g + 2, :], in_=o_sb[:])
 
-        for s in range(NT + LAG + 4):
-            if s % 2 == 0:
-                for i in (s - 4, s - 3):
-                    if 0 <= i < NT:
-                        quant(i)
+        lo = (NV + 1) // 2
+        for s in range(NT + LAG + 5):
+            if s >= QG + 3 and (s - 3) % QG == 0 and (s - 3) // QG - 1 < NT // QG:
+                quant((s - 3) // QG - 1)
+            for k in range(lo):
                 if s < NT:
-                    prod_v(s // 2)
+                    chain_v(s, k)
+                if 0 <= s - 1 < NT and lo + k < NV:
+                    chain_v(s - 1, lo + k)
+            if 0 <= s - 1 < NT:
+                add_g(s - 1)
+            if s < NT:
+                prod_g(s)
+            if 0 <= s - 3 < NT:
+                expo(s - 3)
+            je = s - LAG - 4
+            if je >= 1 and je % 2 == 1 and je < NT:
+                evac(je // 2)
             if s < NT:
                 prod_s(s)
-                prod_g(s)
-            ge = s - LAG - 3
-            if ge >= 0 and ge % 2 == 0 and ge // 2 < NT // 2:
-                evac(ge // 2)
             if 0 <= s - 2 < NT:
-                expo(s - 2)
-            if 0 <= s - 1 < NT:
-                pe_tile(s - 1)
-            elif NT <= s - 1 < NT + LAG:
-                mx_pass(s - 1 - LAG)
+                pe_tile(s - 2)
+            elif NT <= s - 2 < NT + LAG:
+                mx_pass(s - 2 - LAG)

@@ -20,9 +20,9 @@ LN_EPS = 1e-5
 BIG = 3.0e38
 FLOPS = 2 * N * M * POUT
 
-NS = 7
-NG = 1
-NADD = 0
+NS = 6
+NG = 2
+NADD = 1
 NV = 8
 EVN = 2
 REC = 4

@@ -20,10 +20,10 @@ LN_EPS = 1e-5
 BIG = 3.0e38
 FLOPS = 2 * N * M * POUT
 
-NS = 6
+NS = 7
 NG = 2
 NADD = 1
-NV = 8
+NV = 7
 EVN = 2
 REC = 4
 RECP = 4

@@ -20,23 +20,30 @@ LN_EPS = 1e-5
 BIG = 3.0e38
 FLOPS = 2 * N * M * POUT
 
-NS = 7
 NG = 2
+NSF = 6
+SW = NG + NSF
+NVF = D - SW - 1
 NADD = 1
-NV = 7
+SMOD = 2
+SCNT = 1
 EVN = 2
 REC = 4
 RECP = 4
 QG = 4
 LAG = 6
-assert NS + NG + NV == D
-assert 2 * NADD <= NS
+C0 = 8
+NWARM = 0
+LO = 4
+
+
+def s_takes(i):
+    return i % SMOD >= SMOD - SCNT
 
 
 def tile_tmk_t_kernel(tc, x, design_points, chol_inv, out):
     nc = tc.nc
-    nsb2 = (NS + NG + 1) // 2
-    nvb = (NV + 1) // 2
+    nzb = SW + 1
     with ExitStack() as ctx:
         ctx.enter_context(tc.manual_schedule())
         const = ctx.enter_context(tc.tile_pool(name="const", bufs=1))
@@ -47,7 +54,7 @@ def tile_tmk_t_kernel(tc, x, design_points, chol_inv, out):
         cqp = ctx.enter_context(tc.tile_pool(name="cqp", bufs=3))
         osp = ctx.enter_context(tc.tile_pool(name="osp", bufs=3))
         psz = ctx.enter_context(tc.psum_pool(name="psz", bufs=1))
-        psa = ctx.enter_context(tc.psum_pool(name="psa", bufs=8 - 2 - nvb))
+        psa = ctx.enter_context(tc.psum_pool(name="psa", bufs=2))
         pso = ctx.enter_context(tc.psum_pool(name="pso", bufs=2))
 
         z_sb = const.tile([P, PACK, D], BF16)
@@ -57,73 +64,122 @@ def tile_tmk_t_kernel(tc, x, design_points, chol_inv, out):
         w_raw = const.tile([P, PACK, POUT], BF16)
         nc.sync.dma_start(out=w_raw[:], in_=chol_inv.rearrange("(p j) w -> p j w", j=PACK))
 
+        one = const.tile([P, 1], F32)
+        nc.vector.memset(one[:], 1.0)
+        one2 = const.tile([P, 1], F32)
+        nc.scalar.activation(out=one2[:], in_=one[:], func=ACT.Sqrt)
+
         ident_b = const.tile([P, P], BF16)
         make_identity(nc, ident_b[:])
         ident_f = const.tile([P, P], F32)
         make_identity(nc, ident_f[:])
+
+        if NWARM > 0:
+            wz = const.tile([P, M], BF16)
+            nc.vector.memset(wz[:], 0.0)
+            wp = psa.tile([P, M], F32, tag="acc", name="wp")
+            for r in range(NWARM):
+                nc.tensor.matmul(out=wp[:], lhsT=wz[:, 0:P], rhs=wz[:], start=True, stop=True)
 
         zf = const.tile([P, PACK, D], F32)
         nc.vector.tensor_copy(out=zf[:], in_=z_sb[:])
         s_all = const.tile([P, PACK], F32)
         nc.vector.tensor_reduce(out=s_all[:], in_=zf[:], axis=AX.X, op=ALU.add)
         s_sc = const.tile([P, PACK], F32)
-        nc.vector.tensor_reduce(out=s_sc[:], in_=zf[:, :, 0:NS], axis=AX.X, op=ALU.add)
-        cz = const.tile([P, PACK], F32)
-        nc.vector.scalar_tensor_tensor(out=cz[:], in0=s_all[:], scalar=-0.5, in1=s_sc[:], op0=ALU.mult, op1=ALU.add)
+        nc.vector.tensor_reduce(out=s_sc[:], in_=zf[:, :, NG:SW], axis=AX.X, op=ALU.add)
+        cz = const.tile([P, 2, PACK], F32)
+        nc.vector.scalar_tensor_tensor(out=cz[:, 0, :], in0=s_all[:], scalar=-0.5, in1=s_sc[:], op0=ALU.mult, op1=ALU.add)
+        nc.vector.tensor_tensor(out=cz[:, 1, :], in0=cz[:, 0, :], in1=zf[:, :, SW], op=ALU.add)
 
-        w_grp = const.tile([P, POUT, PACK], BF16, align_bytes=64)
-        w_codes = const.tile([P, POUT], U32, align_bytes=64)
-        w_scl = const.tile([P, POUT], U8, align_bytes=64)
-        nc.scalar.copy(out=w_grp[:], in_=w_raw[:].rearrange("p j w -> p w j"))
+        mean = const.tile([P, NT], F32)
+        xc = const.tile([P, NT, D], F32)
+        sq = const.tile([P, NT, D], F32)
+        ve = const.tile([P, NT], F32)
+        sd = const.tile([P, NT], F32)
+        rs = const.tile([P, NT], F32)
+        nw = const.tile([P, NT], F32)
+        xn = const.tile([P, NT, D], F32)
+
+        def ln_mean(a, b):
+            nc.vector.tensor_reduce(out=mean[:, a:b], in_=x_sb[:, a:b, :], axis=AX.X, op=ALU.add)
+            nc.vector.tensor_scalar(out=mean[:, a:b], in0=mean[:, a:b], scalar1=1.0 / D, scalar2=None, op0=ALU.mult)
+
+        def ln_centre(eng, a, b):
+            eng.tensor_tensor(out=xc[:, a:b, :], in0=x_sb[:, a:b, :], in1=mean[:, a:b].unsqueeze(2).to_broadcast([P, b - a, D]), op=ALU.subtract)
+            eng.tensor_tensor(out=sq[:, a:b, :], in0=xc[:, a:b, :], in1=xc[:, a:b, :], op=ALU.mult)
+
+        def ln_var(a, b):
+            nc.vector.tensor_reduce(out=ve[:, a:b], in_=sq[:, a:b, :], axis=AX.X, op=ALU.add)
+            nc.vector.tensor_scalar(out=ve[:, a:b], in0=ve[:, a:b], scalar1=1.0 / D, scalar2=LN_EPS, op0=ALU.mult, op1=ALU.add)
+
+        def ln_sqrt(a, b):
+            nc.scalar.activation(out=sd[:, a:b], in_=ve[:, a:b], func=ACT.Sqrt)
+
+        def ln_rs(a, b):
+            nc.vector.reciprocal(out=rs[:, a:b], in_=sd[:, a:b])
+            nc.vector.tensor_tensor(out=nw[:, a:b], in0=rs[:, a:b], in1=rs[:, a:b], op=ALU.mult)
+            nc.vector.tensor_tensor(out=nw[:, a:b], in0=nw[:, a:b], in1=ve[:, a:b], op=ALU.mult)
+            nc.vector.tensor_scalar(out=nw[:, a:b], in0=nw[:, a:b], scalar1=-0.5, scalar2=1.5, op0=ALU.mult, op1=ALU.add)
+            nc.vector.tensor_tensor(out=rs[:, a:b], in0=rs[:, a:b], in1=nw[:, a:b], op=ALU.mult)
+
+        def ln_scale(eng, a, b):
+            eng.tensor_tensor(out=xn[:, a:b, :], in0=xc[:, a:b, :], in1=rs[:, a:b].unsqueeze(2).to_broadcast([P, b - a, D]), op=ALU.mult)
+
+        ln_mean(0, C0)
+        ln_centre(nc.vector, 0, C0)
+        ln_var(0, C0)
+        ln_sqrt(0, C0)
+        ln_mean(C0, NT)
+        ln_centre(nc.gpsimd, C0, NT)
+        ln_rs(0, C0)
+        ln_scale(nc.vector, 0, C0)
 
         def spread(dst, d, h):
             for t in range(PACK):
                 c0 = h * M + t * P
                 nc.tensor.transpose(dst[:, c0:c0 + P], z_sb[:, t, d:d + 1].to_broadcast([P, P]), ident_b[:])
 
-        zb = const.tile([P, 2 * nsb2, M], BF16)
-        for pair in range(nsb2):
-            tp = psa.tile([P, 2 * M], BF16, tag="acc")
-            for h in range(2):
-                spread(tp, 2 * pair + h, h)
-            nc.scalar.copy(out=zb[:, 2 * pair:2 * pair + 2, :], in_=tp[:].rearrange("p (h m) -> p h m", h=2))
-        zps = []
-        for b in range(nvb):
-            zp = psz.tile([P, 2 * M], BF16, name="zp%d" % b)
-            for h in range(2):
-                if 2 * b + h < NV:
-                    spread(zp, D - NV + 2 * b + h, h)
-            zps.append(zp)
-        cp = psa.tile([P, M], F32, tag="acc")
-        for t in range(PACK):
-            nc.tensor.transpose(cp[:, t * P:(t + 1) * P], cz[:, t:t + 1].to_broadcast([P, P]), ident_f[:])
+        zb = const.tile([P, nzb + nzb % 2, M], BF16)
+        zb_made = set()
 
-        xf = const.tile([P, NT, D], F32)
-        nc.vector.tensor_copy(out=xf[:], in_=x_sb[:])
-        mean = const.tile([P, NT], F32)
-        nc.vector.tensor_reduce(out=mean[:], in_=xf[:], axis=AX.X, op=ALU.add)
-        nc.vector.tensor_scalar(out=mean[:], in0=mean[:], scalar1=1.0 / D, scalar2=None, op0=ALU.mult)
-        xc = const.tile([P, NT, D], F32)
-        nc.vector.tensor_tensor(out=xc[:], in0=xf[:], in1=mean[:].unsqueeze(2).to_broadcast([P, NT, D]), op=ALU.subtract)
-        sq = const.tile([P, NT, D], F32)
-        nc.vector.tensor_tensor(out=sq[:], in0=xc[:], in1=xc[:], op=ALU.mult)
-        ve = const.tile([P, NT], F32)
-        nc.vector.tensor_reduce(out=ve[:], in_=sq[:], axis=AX.X, op=ALU.add)
-        nc.vector.tensor_scalar(out=ve[:], in0=ve[:], scalar1=1.0 / D, scalar2=LN_EPS, op0=ALU.mult, op1=ALU.add)
-        sd = const.tile([P, NT], F32)
-        nc.scalar.activation(out=sd[:], in_=ve[:], func=ACT.Sqrt)
-        nc.vector.quantize_mx(out=w_codes[:].bitcast(FP8X4), scales=w_scl[:], in_=w_grp[:].rearrange("p w j -> p (w j)"))
-        rs = const.tile([P, NT], F32)
-        nc.vector.reciprocal(out=rs[:], in_=sd[:])
-        nw = const.tile([P, NT], F32)
-        nc.vector.tensor_tensor(out=nw[:], in0=rs[:], in1=rs[:], op=ALU.mult)
-        nc.vector.tensor_tensor(out=nw[:], in0=nw[:], in1=ve[:], op=ALU.mult)
-        nc.vector.tensor_scalar(out=nw[:], in0=nw[:], scalar1=-0.5, scalar2=1.5, op0=ALU.mult, op1=ALU.add)
-        nc.vector.tensor_tensor(out=rs[:], in0=rs[:], in1=nw[:], op=ALU.mult)
-        xn = const.tile([P, NT, D], F32)
-        nc.vector.tensor_tensor(out=xn[:], in0=xc[:], in1=rs[:].unsqueeze(2).to_broadcast([P, NT, D]), op=ALU.mult)
-        c_sb = const.tile([P, M], F32)
-        nc.vector.tensor_copy(out=c_sb[:], in_=cp[:])
+        def need_zb(d):
+            pair = d // 2
+            if pair in zb_made:
+                return
+            zb_made.add(pair)
+            nh = min(2, nzb - 2 * pair)
+            tp = psa.tile([P, 2 * M], BF16, tag="acc", name="tp")
+            for h in range(nh):
+                spread(tp, 2 * pair + h, h)
+            nc.scalar.copy(out=zb[:, 2 * pair:2 * pair + nh, :], in_=tp[:, 0:nh * M].rearrange("p (h m) -> p h m", h=nh))
+
+        zps = {}
+
+        def need_zp(k):
+            b = k // 2
+            if b in zps:
+                return
+            zp = psz.tile([P, 2 * M], BF16, name="zp%d" % b)
+            zps[b] = zp
+            for h in range(2):
+                kk = 2 * b + h
+                if kk <= NVF:
+                    spread(zp, SW + 1 + kk if kk < NVF else SW, h)
+
+        c_sb = {}
+
+        def need_c(v):
+            if v in c_sb:
+                return
+            cp = psa.tile([P, M], F32, tag="acc", name="cp")
+            for t in range(PACK):
+                nc.tensor.transpose(cp[:, t * P:(t + 1) * P], cz[:, v, t:t + 1].to_broadcast([P, P]), ident_f[:])
+            c_sb[v] = const.tile([P, M], F32, name="c_sb%d" % v)
+            nc.vector.tensor_copy(out=c_sb[v][:], in_=cp[:])
+
+        w_grp = const.tile([P, POUT, PACK], BF16, align_bytes=64)
+        w_codes = const.tile([P, POUT], U32, align_bytes=64)
+        w_scl = const.tile([P, POUT], U8, align_bytes=64)
 
         out_v = out.rearrange("(p i) c -> p i c", i=NT)
 
@@ -135,18 +191,26 @@ def tile_tmk_t_kernel(tc, x, design_points, chol_inv, out):
         cq_of = {}
         ops_of = {}
 
+        def n_s(i):
+            return NSF + (1 if s_takes(i) else 0)
+
+        def n_v(i):
+            return NVF + (0 if s_takes(i) else 1)
+
         def prod_s(i):
-            ts = tsp.tile([P, NS, M], F32, name="ts")
+            ts = tsp.tile([P, NSF + 1, M], F32, name="ts")
             ts_of[i] = ts
-            for k in range(NS):
-                nc.scalar.activation(out=ts[:, k, :], in_=zb[:, k, :], func=ACT.Relu, bias=xn[:, i, k:k + 1], scale=-1.0)
+            for k in range(n_s(i)):
+                d = NG + k
+                need_zb(d)
+                nc.scalar.activation(out=ts[:, k, :], in_=zb[:, d, :], func=ACT.Relu, bias=xn[:, i, d:d + 1], scale=-1.0)
 
         def prod_g(i):
-            tg = tgp.tile([P, max(NG, 1), M], F32, name="tg")
+            tg = tgp.tile([P, NG, M], F32, name="tg")
             tg_of[i] = tg
-            for k in range(NG):
-                d = NS + k
-                nc.gpsimd.tensor_scalar(out=tg[:, k, :], in0=zb[:, d, :], scalar1=BIG, scalar2=xn[:, i, d:d + 1], op0=ALU.min, op1=ALU.max)
+            for d in range(NG):
+                need_zb(d)
+                nc.gpsimd.tensor_scalar(out=tg[:, d, :], in0=zb[:, d, :], scalar1=BIG, scalar2=xn[:, i, d:d + 1], op0=ALU.min, op1=ALU.max)
 
         def add_g(i):
             ts = ts_of[i]
@@ -154,12 +218,15 @@ def tile_tmk_t_kernel(tc, x, design_points, chol_inv, out):
                 nc.gpsimd.tensor_tensor(out=ts[:, 2 * a, :], in0=ts[:, 2 * a, :], in1=ts[:, 2 * a + 1, :], op=ALU.add)
 
         def chain_v(i, k):
+            v = 1 if s_takes(i) else 0
             if k == 0:
+                need_c(v)
                 tv_of[i] = tvp.tile([P, M], F32, name="tv")
+            need_zp(k)
             tv = tv_of[i]
-            d = NS + NG + k
+            d = SW + 1 + k if k < NVF else SW
             table = zps[k // 2][:, (k % 2) * M:(k % 2 + 1) * M]
-            prev = c_sb if k == 0 else tv
+            prev = c_sb[v] if k == 0 else tv
             nc.vector.scalar_tensor_tensor(
                 out=tv[:], in0=table, scalar=xn[:, i, d:d + 1], in1=prev[:], op0=ALU.max, op1=ALU.add)
 
@@ -183,7 +250,7 @@ def tile_tmk_t_kernel(tc, x, design_points, chol_inv, out):
             terms = [tv_of[i][:]]
             terms += [ts[:, 2 * a, :] for a in range(NADD)]
             terms += [tg_of[i][:, k, :] for k in range(NG)]
-            terms += [ts[:, k, :] for k in range(2 * NADD, NS)]
+            terms += [ts[:, k, :] for k in range(2 * NADD, n_s(i))]
             acc = psa.tile([P, M], F32, tag="acc", name="acc")
             acc_of[i] = acc
             for t in range(PACK):
@@ -217,19 +284,27 @@ def tile_tmk_t_kernel(tc, x, design_points, chol_inv, out):
             nc.scalar.copy(out=o_sb[:], in_=ops_of[g][:].rearrange("p (e c) -> p e c", e=2))
             nc.sync.dma_start(out=out_v[:, 2 * g:2 * g + 2, :], in_=o_sb[:])
 
-        lo = (NV + 1) // 2
         for s in range(NT + LAG + 5):
+            if s == 1:
+                ln_var(C0, NT)
+            if s == 2:
+                ln_rs(C0, NT)
+                nc.vector.quantize_mx(out=w_codes[:].bitcast(FP8X4), scales=w_scl[:], in_=w_grp[:].rearrange("p w j -> p (w j)"))
             if s >= QG + 3 and (s - 3) % QG == 0 and (s - 3) // QG - 1 < NT // QG:
                 quant((s - 3) // QG - 1)
-            for k in range(lo):
+            for k in range(LO):
                 if s < NT:
                     chain_v(s, k)
-                if 0 <= s - 1 < NT and lo + k < NV:
-                    chain_v(s - 1, lo + k)
+                if 0 <= s - 1 < NT and LO + k < n_v(s - 1):
+                    chain_v(s - 1, LO + k)
+            if s == 2:
+                ln_scale(nc.gpsimd, C0, NT)
             if 0 <= s - 1 < NT:
                 add_g(s - 1)
             if s < NT:
                 prod_g(s)
+            if s == 1:
+                ln_sqrt(C0, NT)
             if 0 <= s - 3 < NT:
                 expo(s - 3)
             je = s - LAG - 4
@@ -237,6 +312,8 @@ def tile_tmk_t_kernel(tc, x, design_points, chol_inv, out):
                 evac(je // 2)
             if s < NT:
                 prod_s(s)
+            if s == 0:
+                nc.scalar.copy(out=w_grp[:], in_=w_raw[:].rearrange("p j w -> p w j"))
             if 0 <= s - 2 < NT:
                 pe_tile(s - 2)
             elif NT <= s - 2 < NT + LAG:

@@ -24,21 +24,36 @@ NG = 2
 NSF = 6
 SW = NG + NSF
 NVF = D - SW - 1
+NADD_LAST = 3
 NADD = 1
-SMOD = 2
-SCNT = 1
+PATTERN = "VSG"
+NADD_G = 2
 EVN = 2
 REC = 4
 RECP = 4
 QG = 4
+QSPLIT = True
 LAG = 6
 C0 = 8
 NWARM = 0
+EVMOD = 1000
 LO = 4
 
 
+def q_group(i):
+    if QSPLIT and i >= NT - QG:
+        if i < NT - 2:
+            return NT - QG, 2
+        return i, 1
+    return i - i % QG, QG
+
+
 def s_takes(i):
-    return i % SMOD >= SMOD - SCNT
+    return PATTERN[i % len(PATTERN)] == "S"
+
+
+def g_takes(i):
+    return PATTERN[i % len(PATTERN)] == "G"
 
 
 def tile_tmk_t_kernel(tc, x, design_points, chol_inv, out):
@@ -50,8 +65,8 @@ def tile_tmk_t_kernel(tc, x, design_points, chol_inv, out):
         tsp = ctx.enter_context(tc.tile_pool(name="tsp", bufs=4))
         tgp = ctx.enter_context(tc.tile_pool(name="tgp", bufs=4))
         tvp = ctx.enter_context(tc.tile_pool(name="tvp", bufs=4))
-        kqp = ctx.enter_context(tc.tile_pool(name="kqp", bufs=3))
-        cqp = ctx.enter_context(tc.tile_pool(name="cqp", bufs=3))
+        kqp = ctx.enter_context(tc.tile_pool(name="kqp", bufs=4))
+        cqp = ctx.enter_context(tc.tile_pool(name="cqp", bufs=5))
         osp = ctx.enter_context(tc.tile_pool(name="osp", bufs=3))
         psz = ctx.enter_context(tc.psum_pool(name="psz", bufs=1))
         psa = ctx.enter_context(tc.psum_pool(name="psa", bufs=2))
@@ -175,11 +190,18 @@ def tile_tmk_t_kernel(tc, x, design_points, chol_inv, out):
             for t in range(PACK):
                 nc.tensor.transpose(cp[:, t * P:(t + 1) * P], cz[:, v, t:t + 1].to_broadcast([P, P]), ident_f[:])
             c_sb[v] = const.tile([P, M], F32, name="c_sb%d" % v)
-            nc.vector.tensor_copy(out=c_sb[v][:], in_=cp[:])
+            nc.scalar.copy(out=c_sb[v][:], in_=cp[:])
+
+        need_c(0)
+        need_zp(0)
+        need_zp(2)
+        need_c(1)
 
         w_grp = const.tile([P, POUT, PACK], BF16, align_bytes=64)
         w_codes = const.tile([P, POUT], U32, align_bytes=64)
         w_scl = const.tile([P, POUT], U8, align_bytes=64)
+
+        nc.gpsimd.tensor_scalar(out=w_grp[:], in0=w_raw[:].rearrange("p j w -> p w j"), scalar1=1.0, scalar2=0.0, op0=ALU.mult, op1=ALU.add)
 
         out_v = out.rearrange("(p i) c -> p i c", i=NT)
 
@@ -195,7 +217,10 @@ def tile_tmk_t_kernel(tc, x, design_points, chol_inv, out):
             return NSF + (1 if s_takes(i) else 0)
 
         def n_v(i):
-            return NVF + (0 if s_takes(i) else 1)
+            return NVF + (0 if s_takes(i) or g_takes(i) else 1)
+
+        def n_g(i):
+            return NG + (1 if g_takes(i) else 0)
 
         def prod_s(i):
             ts = tsp.tile([P, NSF + 1, M], F32, name="ts")
@@ -206,15 +231,21 @@ def tile_tmk_t_kernel(tc, x, design_points, chol_inv, out):
                 nc.scalar.activation(out=ts[:, k, :], in_=zb[:, d, :], func=ACT.Relu, bias=xn[:, i, d:d + 1], scale=-1.0)
 
         def prod_g(i):
-            tg = tgp.tile([P, NG, M], F32, name="tg")
+            tg = tgp.tile([P, NG + 1, M], F32, name="tg")
             tg_of[i] = tg
-            for d in range(NG):
+            for k in range(n_g(i)):
+                d = k if k < NG else SW
                 need_zb(d)
-                nc.gpsimd.tensor_scalar(out=tg[:, d, :], in0=zb[:, d, :], scalar1=BIG, scalar2=xn[:, i, d:d + 1], op0=ALU.min, op1=ALU.max)
+                nc.gpsimd.tensor_scalar(out=tg[:, k, :], in0=zb[:, d, :], scalar1=BIG, scalar2=xn[:, i, d:d + 1], op0=ALU.min, op1=ALU.max)
+
+        def n_add(i):
+            if i == NT - 1:
+                return NADD_LAST
+            return NADD_G if g_takes(i) else NADD
 
         def add_g(i):
             ts = ts_of[i]
-            for a in range(NADD):
+            for a in range(n_add(i)):
                 nc.gpsimd.tensor_tensor(out=ts[:, 2 * a, :], in0=ts[:, 2 * a, :], in1=ts[:, 2 * a + 1, :], op=ALU.add)
 
         def chain_v(i, k):
@@ -230,16 +261,20 @@ def tile_tmk_t_kernel(tc, x, design_points, chol_inv, out):
             nc.vector.scalar_tensor_tensor(
                 out=tv[:], in0=table, scalar=xn[:, i, d:d + 1], in1=prev[:], op0=ALU.max, op1=ALU.add)
 
+        def ops_place(j):
+            if QSPLIT and j >= NT - 2:
+                return j - NT // 2 + 1, 0
+            return max(j, 0) // 2, max(j, 0) % 2
+
         def mx_pass(j):
-            g = max(j, 0) // 2
-            e = max(j, 0) % 2
+            g, e = ops_place(j)
             if g not in ops_of:
                 ops_of[g] = pso.tile([P, 2 * POUT], F32, name="ops")
             if j < 0:
                 lhs, lhs_s = w_codes[:, 0:P], w_scl[:, 0:P]
             else:
-                codes, scl = cq_of[j // QG]
-                r = j % QG
+                codes, scl = cq_of[q_group(j)[0]]
+                r = j - q_group(j)[0]
                 lhs, lhs_s = codes[:, r * P:(r + 1) * P], scl[:, r * P:(r + 1) * P]
             nc.tensor.matmul_mx(
                 out=ops_of[g][:, e * POUT:(e + 1) * POUT], lhsT=lhs.bitcast(FP8X4), lhsT_scale=lhs_s,
@@ -248,9 +283,9 @@ def tile_tmk_t_kernel(tc, x, design_points, chol_inv, out):
         def pe_tile(i):
             ts = ts_of[i]
             terms = [tv_of[i][:]]
-            terms += [ts[:, 2 * a, :] for a in range(NADD)]
-            terms += [tg_of[i][:, k, :] for k in range(NG)]
-            terms += [ts[:, k, :] for k in range(2 * NADD, n_s(i))]
+            terms += [ts[:, 2 * a, :] for a in range(n_add(i))]
+            terms += [tg_of[i][:, k, :] for k in range(n_g(i))]
+            terms += [ts[:, k, :] for k in range(2 * n_add(i), n_s(i))]
             acc = psa.tile([P, M], F32, tag="acc", name="acc")
             acc_of[i] = acc
             for t in range(PACK):
@@ -266,22 +301,38 @@ def tile_tmk_t_kernel(tc, x, design_points, chol_inv, out):
                         mx_pass(i - LAG)
 
         def expo(i):
-            if i % QG == 0:
-                kq_of[i // QG] = kqp.tile([P, QG, M], BF16, align_bytes=64, name="kq")
-            kq = kq_of[i // QG]
+            a, n = q_group(i)
+            if i == a:
+                kq_of[a] = kqp.tile([P, QG, M], BF16, align_bytes=64, name="kq")
+            kq = kq_of[a]
             nc.scalar.activation(
-                out=kq[:, i % QG, :].rearrange("p (n t) -> p n t", t=PACK),
+                out=kq[:, i - a, :].rearrange("p (n t) -> p n t", t=PACK),
                 in_=acc_of[i][:].rearrange("p (t n) -> p n t", t=PACK), func=ACT.Exp, scale=-2.0)
 
-        def quant(g):
+        def quant(a, n):
             codes = cqp.tile([P, QG * P], U32, align_bytes=64, name="codes")
             scl = cqp.tile([P, QG * P], U8, align_bytes=64, name="scl")
-            cq_of[g] = (codes, scl)
-            nc.vector.quantize_mx(out=codes[:].bitcast(FP8X4), scales=scl[:], in_=kq_of[g][:].rearrange("p g m -> p (g m)"))
+            cq_of[a] = (codes, scl)
+            nc.vector.quantize_mx(
+                out=codes[:, 0:n * P].bitcast(FP8X4), scales=scl[:, 0:n * P],
+                in_=kq_of[a][:, 0:n, :].rearrange("p g m -> p (g m)"))
+
+        def evac_one(j):
+            o_sb = osp.tile([P, 2, POUT], F32, name="o_sb")
+            g, e = ops_place(j)
+            nc.scalar.copy(out=o_sb[:, e, :], in_=ops_of[g][:, e * POUT:(e + 1) * POUT])
+            nc.sync.dma_start(out=out_v[:, j, :], in_=o_sb[:, e, :])
 
         def evac(g):
+            if QSPLIT and g == NT // 2 - 1:
+                evac_one(2 * g)
+                evac_one(2 * g + 1)
+                return
             o_sb = osp.tile([P, 2, POUT], F32, name="o_sb")
-            nc.scalar.copy(out=o_sb[:], in_=ops_of[g][:].rearrange("p (e c) -> p e c", e=2))
+            if g % EVMOD == EVMOD - 1:
+                nc.vector.tensor_copy(out=o_sb[:], in_=ops_of[g][:].rearrange("p (e c) -> p e c", e=2))
+            else:
+                nc.scalar.copy(out=o_sb[:], in_=ops_of[g][:].rearrange("p (e c) -> p e c", e=2))
             nc.sync.dma_start(out=out_v[:, 2 * g:2 * g + 2, :], in_=o_sb[:])
 
         for s in range(NT + LAG + 5):
@@ -290,8 +341,9 @@ def tile_tmk_t_kernel(tc, x, design_points, chol_inv, out):
             if s == 2:
                 ln_rs(C0, NT)
                 nc.vector.quantize_mx(out=w_codes[:].bitcast(FP8X4), scales=w_scl[:], in_=w_grp[:].rearrange("p w j -> p (w j)"))
-            if s >= QG + 3 and (s - 3) % QG == 0 and (s - 3) // QG - 1 < NT // QG:
-                quant((s - 3) // QG - 1)
+            iq = s - 4
+            if 0 <= iq < NT and iq == sum(q_group(iq)) - 1:
+                quant(q_group(iq)[0], q_group(iq)[1])
             for k in range(LO):
                 if s < NT:
                     chain_v(s, k)
@@ -312,8 +364,6 @@ def tile_tmk_t_kernel(tc, x, design_points, chol_inv, out):
                 evac(je // 2)
             if s < NT:
                 prod_s(s)
-            if s == 0:
-                nc.scalar.copy(out=w_grp[:], in_=w_raw[:].rearrange("p j w -> p w j"))
             if 0 <= s - 2 < NT:
                 pe_tile(s - 2)
             elif NT <= s - 2 < NT + LAG:

@@ -26,7 +26,7 @@ SW = NG + NSF
 NVF = D - SW - 1
 NADD_LAST = 3
 NADD = 1
-PATTERN = "VSG"
+PATTERN = "VSVSG"
 NADD_G = 2
 EVN = 2
 REC = 4

@@ -26,7 +26,7 @@ SW = NG + NSF
 NVF = D - SW - 1
 NADD_LAST = 3
 NADD = 1
-PATTERN = "VSVSG"
+PATTERN = "VSVG"
 NADD_G = 2
 EVN = 2
 REC = 4
@@ -35,7 +35,7 @@ QG = 4
 QSPLIT = True
 LAG = 6
 C0 = 8
-NWARM = 0
+NWARM = 5
 EVMOD = 1000
 LO = 4
 
@@ -140,6 +140,11 @@ def tile_tmk_t_kernel(tc, x, design_points, chol_inv, out):
         def ln_scale(eng, a, b):
             eng.tensor_tensor(out=xn[:, a:b, :], in0=xc[:, a:b, :], in1=rs[:, a:b].unsqueeze(2).to_broadcast([P, b - a, D]), op=ALU.mult)
 
+        w_grp = const.tile([P, POUT, PACK], BF16, align_bytes=64)
+        w_codes = const.tile([P, POUT], U32, align_bytes=64)
+        w_scl = const.tile([P, POUT], U8, align_bytes=64)
+        nc.gpsimd.tensor_scalar(out=w_grp[:], in0=w_raw[:].rearrange("p j w -> p w j"), scalar1=1.0, scalar2=0.0, op0=ALU.mult, op1=ALU.add)
+
         ln_mean(0, C0)
         ln_centre(nc.vector, 0, C0)
         ln_var(0, C0)
@@ -197,11 +202,6 @@ def tile_tmk_t_kernel(tc, x, design_points, chol_inv, out):
         need_zp(2)
         need_c(1)
 
-        w_grp = const.tile([P, POUT, PACK], BF16, align_bytes=64)
-        w_codes = const.tile([P, POUT], U32, align_bytes=64)
-        w_scl = const.tile([P, POUT], U8, align_bytes=64)
-
-        nc.gpsimd.tensor_scalar(out=w_grp[:], in0=w_raw[:].rearrange("p j w -> p w j"), scalar1=1.0, scalar2=0.0, op0=ALU.mult, op1=ALU.add)
 
         out_v = out.rearrange("(p i) c -> p i c", i=NT)
 

@@ -25,9 +25,9 @@ NSF = 6
 SW = NG + NSF
 NVF = D - SW - 1
 NADD_LAST = 3
-NADD = 1
-PATTERN = "VSVG"
-NADD_G = 2
+NADD = 0
+PATTERN = "VGSG"
+NADD_G = 0
 EVN = 2
 REC = 4
 RECP = 4

@@ -28,12 +28,11 @@ NADD_LAST = 3
 NADD = 0
 PATTERN = "VGSG"
 NADD_G = 0
-EVN = 2
-REC = 4
-RECP = 4
+EVA = 3
+EVB = 2
 QG = 4
 QSPLIT = True
-LAG = 6
+LAG = 7
 C0 = 8
 NWARM = 5
 EVMOD = 1000
@@ -62,15 +61,15 @@ def tile_tmk_t_kernel(tc, x, design_points, chol_inv, out):
     with ExitStack() as ctx:
         ctx.enter_context(tc.manual_schedule())
         const = ctx.enter_context(tc.tile_pool(name="const", bufs=1))
-        tsp = ctx.enter_context(tc.tile_pool(name="tsp", bufs=4))
-        tgp = ctx.enter_context(tc.tile_pool(name="tgp", bufs=4))
-        tvp = ctx.enter_context(tc.tile_pool(name="tvp", bufs=4))
+        tsp = ctx.enter_context(tc.tile_pool(name="tsp", bufs=5))
+        tgp = ctx.enter_context(tc.tile_pool(name="tgp", bufs=5))
+        tvp = ctx.enter_context(tc.tile_pool(name="tvp", bufs=5))
         kqp = ctx.enter_context(tc.tile_pool(name="kqp", bufs=4))
         cqp = ctx.enter_context(tc.tile_pool(name="cqp", bufs=5))
         osp = ctx.enter_context(tc.tile_pool(name="osp", bufs=3))
         psz = ctx.enter_context(tc.psum_pool(name="psz", bufs=1))
-        psa = ctx.enter_context(tc.psum_pool(name="psa", bufs=2))
-        pso = ctx.enter_context(tc.psum_pool(name="pso", bufs=2))
+        psa = ctx.enter_context(tc.psum_pool(name="psa", bufs=3))
+        pso = ctx.enter_context(tc.psum_pool(name="pso", bufs=1))
 
         z_sb = const.tile([P, PACK, D], BF16)
         nc.sync.dma_start(out=z_sb[:], in_=design_points.rearrange("(p t) d -> p t d", t=PACK))
@@ -266,10 +265,15 @@ def tile_tmk_t_kernel(tc, x, design_points, chol_inv, out):
                 return j - NT // 2 + 1, 0
             return max(j, 0) // 2, max(j, 0) % 2
 
-        def mx_pass(j):
-            g, e = ops_place(j)
-            if g not in ops_of:
-                ops_of[g] = pso.tile([P, 2 * POUT], F32, name="ops")
+        def mx_pass(j, dst=None):
+            if dst is None:
+                g, e = ops_place(j)
+                if g not in ops_of:
+                    if QSPLIT and j >= NT - 2:
+                        ops_of[g] = psa.tile([P, 2 * POUT], F32, tag="acc", name="ops_end")
+                    else:
+                        ops_of[g] = pso.tile([P, 2 * POUT], F32, name="ops")
+                dst = ops_of[g][:, e * POUT:(e + 1) * POUT]
             if j < 0:
                 lhs, lhs_s = w_codes[:, 0:P], w_scl[:, 0:P]
             else:
@@ -277,27 +281,36 @@ def tile_tmk_t_kernel(tc, x, design_points, chol_inv, out):
                 r = j - q_group(j)[0]
                 lhs, lhs_s = codes[:, r * P:(r + 1) * P], scl[:, r * P:(r + 1) * P]
             nc.tensor.matmul_mx(
-                out=ops_of[g][:, e * POUT:(e + 1) * POUT], lhsT=lhs.bitcast(FP8X4), lhsT_scale=lhs_s,
+                out=dst, lhsT=lhs.bitcast(FP8X4), lhsT_scale=lhs_s,
                 rhs=w_codes[:].bitcast(FP8X4), rhs_scale=w_scl[:], start=True, stop=True)
 
-        def pe_tile(i):
+        def terms_of(i):
             ts = ts_of[i]
             terms = [tv_of[i][:]]
             terms += [ts[:, 2 * a, :] for a in range(n_add(i))]
             terms += [tg_of[i][:, k, :] for k in range(n_g(i))]
             terms += [ts[:, k, :] for k in range(2 * n_add(i), n_s(i))]
-            acc = psa.tile([P, M], F32, tag="acc", name="acc")
-            acc_of[i] = acc
-            for t in range(PACK):
-                for q, term in enumerate(terms):
-                    nc.tensor.matmul(
-                        out=acc[:, t * P:(t + 1) * P], lhsT=term[:, t * P:(t + 1) * P], rhs=ident_f[:],
-                        is_transpose=True, start=(q == 0), stop=(q == len(terms) - 1))
-                if t % 2 == 1:
-                    n = EVN
-                    if t == 1 and i % RECP == 0:
-                        n = EVN + REC
-                    for r in range(n):
+            return terms
+
+        def slot(i):
+            if i < NT:
+                acc_of[i] = psa.tile([P, M], F32, tag="acc", name="acc")
+                for r in range(EVA):
+                    mx_pass(i - LAG, dst=acc_of[i][:, 0:POUT])
+            for h in range(2):
+                jobs = []
+                if i >= 1:
+                    jobs.append((acc_of[i - 1], 2 + h, terms_of(i - 1)))
+                if i < NT:
+                    jobs.append((acc_of[i], h, terms_of(i)))
+                for q in range(max(len(job[2]) for job in jobs)):
+                    for acc, t, terms in jobs:
+                        if q < len(terms):
+                            nc.tensor.matmul(
+                                out=acc[:, t * P:(t + 1) * P], lhsT=terms[q][:, t * P:(t + 1) * P], rhs=ident_f[:],
+                                is_transpose=True, start=(q == 0), stop=(q == len(terms) - 1))
+                if h == 0:
+                    for r in range(EVB):
                         mx_pass(i - LAG)
 
         def expo(i):
@@ -335,13 +348,13 @@ def tile_tmk_t_kernel(tc, x, design_points, chol_inv, out):
                 nc.scalar.copy(out=o_sb[:], in_=ops_of[g][:].rearrange("p (e c) -> p e c", e=2))
             nc.sync.dma_start(out=out_v[:, 2 * g:2 * g + 2, :], in_=o_sb[:])
 
-        for s in range(NT + LAG + 5):
+        for s in range(NT + LAG + 4):
             if s == 1:
                 ln_var(C0, NT)
             if s == 2:
                 ln_rs(C0, NT)
                 nc.vector.quantize_mx(out=w_codes[:].bitcast(FP8X4), scales=w_scl[:], in_=w_grp[:].rearrange("p w j -> p (w j)"))
-            iq = s - 4
+            iq = s - 5
             if 0 <= iq < NT and iq == sum(q_group(iq)) - 1:
                 quant(q_group(iq)[0], q_group(iq)[1])
             for k in range(LO):
@@ -357,14 +370,14 @@ def tile_tmk_t_kernel(tc, x, design_points, chol_inv, out):
                 prod_g(s)
             if s == 1:
                 ln_sqrt(C0, NT)
-            if 0 <= s - 3 < NT:
-                expo(s - 3)
-            je = s - LAG - 4
+            if 0 <= s - 4 < NT:
+                expo(s - 4)
+            je = s - LAG - 3
             if je >= 1 and je % 2 == 1 and je < NT:
                 evac(je // 2)
             if s < NT:
                 prod_s(s)
-            if 0 <= s - 2 < NT:
-                pe_tile(s - 2)
-            elif NT <= s - 2 < NT + LAG:
+            if 0 <= s - 2 <= NT:
+                slot(s - 2)
+            elif NT < s - 2 < NT + LAG:
                 mx_pass(s - 2 - LAG)

@@ -20,13 +20,13 @@ LN_EPS = 1e-5
 BIG = 3.0e38
 FLOPS = 2 * N * M * POUT
 
-NG = 2
+NG = 3
 NSF = 6
 SW = NG + NSF
 NVF = D - SW - 1
 NADD_LAST = 3
-NADD = 0
-PATTERN = "VGSG"
+NADD = 1
+PATTERN = "V"
 NADD_G = 0
 EVA = 3
 EVB = 2
@@ -57,7 +57,7 @@ def g_takes(i):
 
 def tile_tmk_t_kernel(tc, x, design_points, chol_inv, out):
     nc = tc.nc
-    nzb = SW + 1
+    nzb = SW
     with ExitStack() as ctx:
         ctx.enter_context(tc.manual_schedule())
         const = ctx.enter_context(tc.tile_pool(name="const", bufs=1))
@@ -103,7 +103,6 @@ def tile_tmk_t_kernel(tc, x, design_points, chol_inv, out):
         nc.vector.tensor_reduce(out=s_sc[:], in_=zf[:, :, NG:SW], axis=AX.X, op=ALU.add)
         cz = const.tile([P, 2, PACK], F32)
         nc.vector.scalar_tensor_tensor(out=cz[:, 0, :], in0=s_all[:], scalar=-0.5, in1=s_sc[:], op0=ALU.mult, op1=ALU.add)
-        nc.vector.tensor_tensor(out=cz[:, 1, :], in0=cz[:, 0, :], in1=zf[:, :, SW], op=ALU.add)
 
         mean = const.tile([P, NT], F32)
         xc = const.tile([P, NT, D], F32)
@@ -199,7 +198,6 @@ def tile_tmk_t_kernel(tc, x, design_points, chol_inv, out):
         need_c(0)
         need_zp(0)
         need_zp(2)
-        need_c(1)
 
 
         out_v = out.rearrange("(p i) c -> p i c", i=NT)
@@ -295,7 +293,7 @@ def tile_tmk_t_kernel(tc, x, design_points, chol_inv, out):
         def slot(i):
             if i < NT:
                 acc_of[i] = psa.tile([P, M], F32, tag="acc", name="acc")
-                for r in range(EVA):
+                for r in range(EVA if i >= 3 else 0):
                     mx_pass(i - LAG, dst=acc_of[i][:, 0:POUT])
             for h in range(2):
                 jobs = []
@@ -310,7 +308,7 @@ def tile_tmk_t_kernel(tc, x, design_points, chol_inv, out):
                                 out=acc[:, t * P:(t + 1) * P], lhsT=terms[q][:, t * P:(t + 1) * P], rhs=ident_f[:],
                                 is_transpose=True, start=(q == 0), stop=(q == len(terms) - 1))
                 if h == 0:
-                    for r in range(EVB):
+                    for r in range(EVB if i >= 3 else 0):
                         mx_pass(i - LAG)
 
         def expo(i):

@@ -21,43 +21,40 @@ BIG = 3.0e38
 FLOPS = 2 * N * M * POUT
 
 NG = 3
-NSF = 6
-SW = NG + NSF
-NVF = D - SW - 1
-NADD_LAST = 3
+NS = 6
+V0 = NG + NS
+NV = D - V0
 NADD = 1
-PATTERN = "V"
-NADD_G = 0
-EVA = 3
+EVA = 2
 EVB = 2
 QG = 4
-QSPLIT = True
 LAG = 7
 C0 = 8
 NWARM = 5
-EVMOD = 1000
 LO = 4
+FIRST_EV = 3
 
 
 def q_group(i):
-    if QSPLIT and i >= NT - QG:
+    if i >= NT - QG:
         if i < NT - 2:
             return NT - QG, 2
         return i, 1
     return i - i % QG, QG
 
 
-def s_takes(i):
-    return PATTERN[i % len(PATTERN)] == "S"
-
-
-def g_takes(i):
-    return PATTERN[i % len(PATTERN)] == "G"
+def result_slot(j):
+    if j >= NT - 2:
+        return j + 4
+    if j >= NT - 4:
+        return NT + 1
+    if j >= NT - 8:
+        return NT - 1
+    return j + LAG
 
 
 def tile_tmk_t_kernel(tc, x, design_points, chol_inv, out):
     nc = tc.nc
-    nzb = SW
     with ExitStack() as ctx:
         ctx.enter_context(tc.manual_schedule())
         const = ctx.enter_context(tc.tile_pool(name="const", bufs=1))
@@ -66,15 +63,17 @@ def tile_tmk_t_kernel(tc, x, design_points, chol_inv, out):
         tvp = ctx.enter_context(tc.tile_pool(name="tvp", bufs=5))
         kqp = ctx.enter_context(tc.tile_pool(name="kqp", bufs=4))
         cqp = ctx.enter_context(tc.tile_pool(name="cqp", bufs=5))
-        osp = ctx.enter_context(tc.tile_pool(name="osp", bufs=3))
+        osp = ctx.enter_context(tc.tile_pool(name="osp", bufs=4))
         psz = ctx.enter_context(tc.psum_pool(name="psz", bufs=1))
         psa = ctx.enter_context(tc.psum_pool(name="psa", bufs=3))
         pso = ctx.enter_context(tc.psum_pool(name="pso", bufs=1))
 
-        z_sb = const.tile([P, PACK, D], BF16)
-        nc.sync.dma_start(out=z_sb[:], in_=design_points.rearrange("(p t) d -> p t d", t=PACK))
+        x_v = x.rearrange("(p i) d -> p i d", i=NT)
         x_sb = const.tile([P, NT, D], BF16)
-        nc.sync.dma_start(out=x_sb[:], in_=x.rearrange("(p i) d -> p i d", i=NT))
+        nc.sync.dma_start(out=x_sb[:, 0:C0, :], in_=x_v[:, 0:C0, :])
+        z_sb = const.tile([P, PACK, D], BF16)
+        nc.scalar.dma_start(out=z_sb[:], in_=design_points.rearrange("(p t) d -> p t d", t=PACK))
+        nc.sync.dma_start(out=x_sb[:, C0:NT, :], in_=x_v[:, C0:NT, :])
         w_raw = const.tile([P, PACK, POUT], BF16)
         nc.sync.dma_start(out=w_raw[:], in_=chol_inv.rearrange("(p j) w -> p j w", j=PACK))
 
@@ -88,42 +87,34 @@ def tile_tmk_t_kernel(tc, x, design_points, chol_inv, out):
         ident_f = const.tile([P, P], F32)
         make_identity(nc, ident_f[:])
 
-        if NWARM > 0:
-            wz = const.tile([P, M], BF16)
-            nc.vector.memset(wz[:], 0.0)
-            wp = psa.tile([P, M], F32, tag="acc", name="wp")
-            for r in range(NWARM):
-                nc.tensor.matmul(out=wp[:], lhsT=wz[:, 0:P], rhs=wz[:], start=True, stop=True)
+        wz = const.tile([P, M], BF16)
+        nc.vector.memset(wz[:], 0.0)
+        wp = psa.tile([P, M], F32, tag="acc", name="wp")
+        for r in range(NWARM):
+            nc.tensor.matmul(out=wp[:], lhsT=wz[:, 0:P], rhs=wz[:], start=True, stop=True)
 
-        zf = const.tile([P, PACK, D], F32)
-        nc.vector.tensor_copy(out=zf[:], in_=z_sb[:])
-        s_all = const.tile([P, PACK], F32)
-        nc.vector.tensor_reduce(out=s_all[:], in_=zf[:], axis=AX.X, op=ALU.add)
-        s_sc = const.tile([P, PACK], F32)
-        nc.vector.tensor_reduce(out=s_sc[:], in_=zf[:, :, NG:SW], axis=AX.X, op=ALU.add)
-        cz = const.tile([P, 2, PACK], F32)
-        nc.vector.scalar_tensor_tensor(out=cz[:, 0, :], in0=s_all[:], scalar=-0.5, in1=s_sc[:], op0=ALU.mult, op1=ALU.add)
-
-        mean = const.tile([P, NT], F32)
+        sm = const.tile([P, NT], F32)
         xc = const.tile([P, NT, D], F32)
         sq = const.tile([P, NT, D], F32)
+        ss = const.tile([P, NT], F32)
         ve = const.tile([P, NT], F32)
         sd = const.tile([P, NT], F32)
         rs = const.tile([P, NT], F32)
         nw = const.tile([P, NT], F32)
         xn = const.tile([P, NT, D], F32)
+        s_all = const.tile([P, PACK], F32)
+        s_sc = const.tile([P, PACK], F32)
+        cz = const.tile([P, PACK], F32)
 
-        def ln_mean(a, b):
-            nc.vector.tensor_reduce(out=mean[:, a:b], in_=x_sb[:, a:b, :], axis=AX.X, op=ALU.add)
-            nc.vector.tensor_scalar(out=mean[:, a:b], in0=mean[:, a:b], scalar1=1.0 / D, scalar2=None, op0=ALU.mult)
+        def wide(t, a, b):
+            return t[:, a:b].unsqueeze(2).to_broadcast([P, b - a, D])
 
-        def ln_centre(eng, a, b):
-            eng.tensor_tensor(out=xc[:, a:b, :], in0=x_sb[:, a:b, :], in1=mean[:, a:b].unsqueeze(2).to_broadcast([P, b - a, D]), op=ALU.subtract)
-            eng.tensor_tensor(out=sq[:, a:b, :], in0=xc[:, a:b, :], in1=xc[:, a:b, :], op=ALU.mult)
+        def ln_sum(a, b):
+            nc.vector.tensor_reduce(out=sm[:, a:b], in_=x_sb[:, a:b, :], axis=AX.X, op=ALU.add)
 
         def ln_var(a, b):
-            nc.vector.tensor_reduce(out=ve[:, a:b], in_=sq[:, a:b, :], axis=AX.X, op=ALU.add)
-            nc.vector.tensor_scalar(out=ve[:, a:b], in0=ve[:, a:b], scalar1=1.0 / D, scalar2=LN_EPS, op0=ALU.mult, op1=ALU.add)
+            nc.vector.tensor_reduce(out=ss[:, a:b], in_=sq[:, a:b, :], axis=AX.X, op=ALU.add)
+            nc.vector.tensor_scalar(out=ve[:, a:b], in0=ss[:, a:b], scalar1=1.0 / D, scalar2=LN_EPS, op0=ALU.mult, op1=ALU.add)
 
         def ln_sqrt(a, b):
             nc.scalar.activation(out=sd[:, a:b], in_=ve[:, a:b], func=ACT.Sqrt)
@@ -131,33 +122,35 @@ def tile_tmk_t_kernel(tc, x, design_points, chol_inv, out):
         def ln_rs(a, b):
             nc.vector.reciprocal(out=rs[:, a:b], in_=sd[:, a:b])
             nc.vector.tensor_tensor(out=nw[:, a:b], in0=rs[:, a:b], in1=rs[:, a:b], op=ALU.mult)
-            nc.vector.tensor_tensor(out=nw[:, a:b], in0=nw[:, a:b], in1=ve[:, a:b], op=ALU.mult)
-            nc.vector.tensor_scalar(out=nw[:, a:b], in0=nw[:, a:b], scalar1=-0.5, scalar2=1.5, op0=ALU.mult, op1=ALU.add)
-            nc.vector.tensor_tensor(out=rs[:, a:b], in0=rs[:, a:b], in1=nw[:, a:b], op=ALU.mult)
+            nc.vector.scalar_tensor_tensor(out=nw[:, a:b], in0=nw[:, a:b], scalar=-0.5, in1=ve[:, a:b], op0=ALU.mult, op1=ALU.mult)
+            nc.vector.scalar_tensor_tensor(out=rs[:, a:b], in0=nw[:, a:b], scalar=1.5, in1=rs[:, a:b], op0=ALU.add, op1=ALU.mult)
 
-        def ln_scale(eng, a, b):
-            eng.tensor_tensor(out=xn[:, a:b, :], in0=xc[:, a:b, :], in1=rs[:, a:b].unsqueeze(2).to_broadcast([P, b - a, D]), op=ALU.mult)
+        ln_sum(0, C0)
+        nc.vector.tensor_reduce(out=s_all[:], in_=z_sb[:], axis=AX.X, op=ALU.add)
+        nc.vector.scalar_tensor_tensor(out=xc[:, 0:C0, :], in0=wide(sm, 0, C0), scalar=-1.0 / D, in1=x_sb[:, 0:C0, :], op0=ALU.mult, op1=ALU.add)
+        nc.vector.tensor_reduce(out=s_sc[:], in_=z_sb[:, :, NG:V0], axis=AX.X, op=ALU.add)
+        nc.vector.tensor_tensor(out=sq[:, 0:C0, :], in0=xc[:, 0:C0, :], in1=xc[:, 0:C0, :], op=ALU.mult)
+        nc.vector.scalar_tensor_tensor(out=cz[:], in0=s_all[:], scalar=-0.5, in1=s_sc[:], op0=ALU.mult, op1=ALU.add)
+        ln_var(0, C0)
+        ln_sqrt(0, C0)
+        ln_rs(0, C0)
+        nc.vector.tensor_tensor(out=xn[:, 0:C0, :], in0=xc[:, 0:C0, :], in1=wide(rs, 0, C0), op=ALU.mult)
+        ln_sum(C0, NT)
+        nc.vector.tensor_scalar(out=sm[:, C0:NT], in0=sm[:, C0:NT], scalar1=1.0 / D, scalar2=None, op0=ALU.mult)
 
         w_grp = const.tile([P, POUT, PACK], BF16, align_bytes=64)
         w_codes = const.tile([P, POUT], U32, align_bytes=64)
         w_scl = const.tile([P, POUT], U8, align_bytes=64)
         nc.gpsimd.tensor_scalar(out=w_grp[:], in0=w_raw[:].rearrange("p j w -> p w j"), scalar1=1.0, scalar2=0.0, op0=ALU.mult, op1=ALU.add)
-
-        ln_mean(0, C0)
-        ln_centre(nc.vector, 0, C0)
-        ln_var(0, C0)
-        ln_sqrt(0, C0)
-        ln_mean(C0, NT)
-        ln_centre(nc.gpsimd, C0, NT)
-        ln_rs(0, C0)
-        ln_scale(nc.vector, 0, C0)
+        nc.gpsimd.tensor_tensor(out=xc[:, C0:NT, :], in0=x_sb[:, C0:NT, :], in1=wide(sm, C0, NT), op=ALU.subtract)
+        nc.gpsimd.tensor_tensor(out=sq[:, C0:NT, :], in0=xc[:, C0:NT, :], in1=xc[:, C0:NT, :], op=ALU.mult)
 
         def spread(dst, d, h):
             for t in range(PACK):
                 c0 = h * M + t * P
                 nc.tensor.transpose(dst[:, c0:c0 + P], z_sb[:, t, d:d + 1].to_broadcast([P, P]), ident_b[:])
 
-        zb = const.tile([P, nzb + nzb % 2, M], BF16)
+        zb = const.tile([P, V0 + V0 % 2, M], BF16)
         zb_made = set()
 
         def need_zb(d):
@@ -165,7 +158,7 @@ def tile_tmk_t_kernel(tc, x, design_points, chol_inv, out):
             if pair in zb_made:
                 return
             zb_made.add(pair)
-            nh = min(2, nzb - 2 * pair)
+            nh = min(2, V0 - 2 * pair)
             tp = psa.tile([P, 2 * M], BF16, tag="acc", name="tp")
             for h in range(nh):
                 spread(tp, 2 * pair + h, h)
@@ -179,26 +172,16 @@ def tile_tmk_t_kernel(tc, x, design_points, chol_inv, out):
                 return
             zp = psz.tile([P, 2 * M], BF16, name="zp%d" % b)
             zps[b] = zp
-            for h in range(2):
-                kk = 2 * b + h
-                if kk <= NVF:
-                    spread(zp, SW + 1 + kk if kk < NVF else SW, h)
+            for h in range(min(2, NV - 2 * b)):
+                spread(zp, V0 + 2 * b + h, h)
 
-        c_sb = {}
-
-        def need_c(v):
-            if v in c_sb:
-                return
-            cp = psa.tile([P, M], F32, tag="acc", name="cp")
-            for t in range(PACK):
-                nc.tensor.transpose(cp[:, t * P:(t + 1) * P], cz[:, v, t:t + 1].to_broadcast([P, P]), ident_f[:])
-            c_sb[v] = const.tile([P, M], F32, name="c_sb%d" % v)
-            nc.scalar.copy(out=c_sb[v][:], in_=cp[:])
-
-        need_c(0)
+        cp = psa.tile([P, M], F32, tag="acc", name="cp")
+        c_sb = const.tile([P, M], F32)
         need_zp(0)
+        for t in range(PACK):
+            nc.tensor.transpose(cp[:, t * P:(t + 1) * P], cz[:, t:t + 1].to_broadcast([P, P]), ident_f[:])
+        nc.scalar.copy(out=c_sb[:], in_=cp[:])
         need_zp(2)
-
 
         out_v = out.rearrange("(p i) c -> p i c", i=NT)
 
@@ -210,68 +193,42 @@ def tile_tmk_t_kernel(tc, x, design_points, chol_inv, out):
         cq_of = {}
         ops_of = {}
 
-        def n_s(i):
-            return NSF + (1 if s_takes(i) else 0)
-
-        def n_v(i):
-            return NVF + (0 if s_takes(i) or g_takes(i) else 1)
-
-        def n_g(i):
-            return NG + (1 if g_takes(i) else 0)
-
         def prod_s(i):
-            ts = tsp.tile([P, NSF + 1, M], F32, name="ts")
+            ts = tsp.tile([P, NS, M], F32, name="ts")
             ts_of[i] = ts
-            for k in range(n_s(i)):
+            for k in range(NS):
                 d = NG + k
                 need_zb(d)
                 nc.scalar.activation(out=ts[:, k, :], in_=zb[:, d, :], func=ACT.Relu, bias=xn[:, i, d:d + 1], scale=-1.0)
 
         def prod_g(i):
-            tg = tgp.tile([P, NG + 1, M], F32, name="tg")
+            tg = tgp.tile([P, NG, M], F32, name="tg")
             tg_of[i] = tg
-            for k in range(n_g(i)):
-                d = k if k < NG else SW
+            for d in range(NG):
                 need_zb(d)
-                nc.gpsimd.tensor_scalar(out=tg[:, k, :], in0=zb[:, d, :], scalar1=BIG, scalar2=xn[:, i, d:d + 1], op0=ALU.min, op1=ALU.max)
-
-        def n_add(i):
-            if i == NT - 1:
-                return NADD_LAST
-            return NADD_G if g_takes(i) else NADD
+                nc.gpsimd.tensor_scalar(out=tg[:, d, :], in0=zb[:, d, :], scalar1=BIG, scalar2=xn[:, i, d:d + 1], op0=ALU.min, op1=ALU.max)
 
         def add_g(i):
             ts = ts_of[i]
-            for a in range(n_add(i)):
+            for a in range(NADD):
                 nc.gpsimd.tensor_tensor(out=ts[:, 2 * a, :], in0=ts[:, 2 * a, :], in1=ts[:, 2 * a + 1, :], op=ALU.add)
 
         def chain_v(i, k):
-            v = 1 if s_takes(i) else 0
             if k == 0:
-                need_c(v)
                 tv_of[i] = tvp.tile([P, M], F32, name="tv")
             need_zp(k)
             tv = tv_of[i]
-            d = SW + 1 + k if k < NVF else SW
             table = zps[k // 2][:, (k % 2) * M:(k % 2 + 1) * M]
-            prev = c_sb[v] if k == 0 else tv
+            prev = c_sb if k == 0 else tv
             nc.vector.scalar_tensor_tensor(
-                out=tv[:], in0=table, scalar=xn[:, i, d:d + 1], in1=prev[:], op0=ALU.max, op1=ALU.add)
+                out=tv[:], in0=table, scalar=xn[:, i, V0 + k:V0 + k + 1], in1=prev[:], op0=ALU.max, op1=ALU.add)
 
         def ops_place(j):
-            if QSPLIT and j >= NT - 2:
+            if j >= NT - 2:
                 return j - NT // 2 + 1, 0
-            return max(j, 0) // 2, max(j, 0) % 2
+            return j // 2, j % 2
 
-        def mx_pass(j, dst=None):
-            if dst is None:
-                g, e = ops_place(j)
-                if g not in ops_of:
-                    if QSPLIT and j >= NT - 2:
-                        ops_of[g] = psa.tile([P, 2 * POUT], F32, tag="acc", name="ops_end")
-                    else:
-                        ops_of[g] = pso.tile([P, 2 * POUT], F32, name="ops")
-                dst = ops_of[g][:, e * POUT:(e + 1) * POUT]
+        def mx(j, dst):
             if j < 0:
                 lhs, lhs_s = w_codes[:, 0:P], w_scl[:, 0:P]
             else:
@@ -282,19 +239,29 @@ def tile_tmk_t_kernel(tc, x, design_points, chol_inv, out):
                 out=dst, lhsT=lhs.bitcast(FP8X4), lhsT_scale=lhs_s,
                 rhs=w_codes[:].bitcast(FP8X4), rhs_scale=w_scl[:], start=True, stop=True)
 
+        def result(j):
+            g, e = ops_place(j)
+            if g not in ops_of:
+                if j >= NT - 2 or NT - 6 <= j < NT - 4:
+                    ops_of[g] = psa.tile([P, 2 * POUT], F32, tag="acc", name="ops_end")
+                else:
+                    ops_of[g] = pso.tile([P, 2 * POUT], F32, name="ops")
+            mx(j, ops_of[g][:, e * POUT:(e + 1) * POUT])
+
         def terms_of(i):
             ts = ts_of[i]
-            terms = [tv_of[i][:]]
-            terms += [ts[:, 2 * a, :] for a in range(n_add(i))]
-            terms += [tg_of[i][:, k, :] for k in range(n_g(i))]
-            terms += [ts[:, k, :] for k in range(2 * n_add(i), n_s(i))]
+            terms = [ts[:, k, :] for k in range(2 * NADD, NS)]
+            terms += [tg_of[i][:, k, :] for k in range(NG)]
+            terms += [ts[:, 2 * a, :] for a in range(NADD)]
+            terms.append(tv_of[i][:])
             return terms
 
         def slot(i):
             if i < NT:
                 acc_of[i] = psa.tile([P, M], F32, tag="acc", name="acc")
-                for r in range(EVA if i >= 3 else 0):
-                    mx_pass(i - LAG, dst=acc_of[i][:, 0:POUT])
+                if FIRST_EV <= i < NT - 1:
+                    for r in range(EVA):
+                        mx(i - LAG, acc_of[i][:, 0:POUT])
             for h in range(2):
                 jobs = []
                 if i >= 1:
@@ -303,13 +270,22 @@ def tile_tmk_t_kernel(tc, x, design_points, chol_inv, out):
                     jobs.append((acc_of[i], h, terms_of(i)))
                 for q in range(max(len(job[2]) for job in jobs)):
                     for acc, t, terms in jobs:
-                        if q < len(terms):
-                            nc.tensor.matmul(
-                                out=acc[:, t * P:(t + 1) * P], lhsT=terms[q][:, t * P:(t + 1) * P], rhs=ident_f[:],
-                                is_transpose=True, start=(q == 0), stop=(q == len(terms) - 1))
+                        nc.tensor.matmul(
+                            out=acc[:, t * P:(t + 1) * P], lhsT=terms[q][:, t * P:(t + 1) * P], rhs=ident_f[:],
+                            is_transpose=True, start=(q == 0), stop=(q == len(terms) - 1))
                 if h == 0:
-                    for r in range(EVB if i >= 3 else 0):
-                        mx_pass(i - LAG)
+                    results(i)
+
+        def results(i):
+            made = [j for j in range(max(0, i - LAG), NT) if result_slot(j) == i]
+            for j in made:
+                result(j)
+            if FIRST_EV <= i < NT - 1:
+                for r in range(EVB - len(made)):
+                    g, e = ops_place(max(0, i - LAG))
+                    if g not in ops_of:
+                        ops_of[g] = pso.tile([P, 2 * POUT], F32, name="ops")
+                    mx(i - LAG, ops_of[g][:, e * POUT:(e + 1) * POUT])
 
         def expo(i):
             a, n = q_group(i)
@@ -328,25 +304,13 @@ def tile_tmk_t_kernel(tc, x, design_points, chol_inv, out):
                 out=codes[:, 0:n * P].bitcast(FP8X4), scales=scl[:, 0:n * P],
                 in_=kq_of[a][:, 0:n, :].rearrange("p g m -> p (g m)"))
 
-        def evac_one(j):
+        def evac(j0, n, copy):
             o_sb = osp.tile([P, 2, POUT], F32, name="o_sb")
-            g, e = ops_place(j)
-            nc.scalar.copy(out=o_sb[:, e, :], in_=ops_of[g][:, e * POUT:(e + 1) * POUT])
-            nc.sync.dma_start(out=out_v[:, j, :], in_=o_sb[:, e, :])
+            src = ops_of[ops_place(j0)[0]][:, 0:n * POUT]
+            copy(out=o_sb[:, 0:n, :], in_=src.rearrange("p (e c) -> p e c", e=n))
+            nc.sync.dma_start(out=out_v[:, j0:j0 + n, :], in_=o_sb[:, 0:n, :])
 
-        def evac(g):
-            if QSPLIT and g == NT // 2 - 1:
-                evac_one(2 * g)
-                evac_one(2 * g + 1)
-                return
-            o_sb = osp.tile([P, 2, POUT], F32, name="o_sb")
-            if g % EVMOD == EVMOD - 1:
-                nc.vector.tensor_copy(out=o_sb[:], in_=ops_of[g][:].rearrange("p (e c) -> p e c", e=2))
-            else:
-                nc.scalar.copy(out=o_sb[:], in_=ops_of[g][:].rearrange("p (e c) -> p e c", e=2))
-            nc.sync.dma_start(out=out_v[:, 2 * g:2 * g + 2, :], in_=o_sb[:])
-
-        for s in range(NT + LAG + 4):
+        for s in range(NT + 7):
             if s == 1:
                 ln_var(C0, NT)
             if s == 2:
@@ -355,27 +319,35 @@ def tile_tmk_t_kernel(tc, x, design_points, chol_inv, out):
             iq = s - 5
             if 0 <= iq < NT and iq == sum(q_group(iq)) - 1:
                 quant(q_group(iq)[0], q_group(iq)[1])
-            for k in range(LO):
-                if s < NT:
+            for k in range(max(LO, NV - LO)):
+                if s < NT and k < LO:
                     chain_v(s, k)
-                if 0 <= s - 1 < NT and LO + k < n_v(s - 1):
+                if 0 <= s - 1 < NT and LO + k < NV:
                     chain_v(s - 1, LO + k)
             if s == 2:
-                ln_scale(nc.gpsimd, C0, NT)
+                nc.gpsimd.tensor_tensor(out=xn[:, C0:NT, :], in0=xc[:, C0:NT, :], in1=wide(rs, C0, NT), op=ALU.mult)
             if 0 <= s - 1 < NT:
                 add_g(s - 1)
             if s < NT:
                 prod_g(s)
             if s == 1:
                 ln_sqrt(C0, NT)
+            if s == NT + 2:
+                evac(NT - 8, 2, nc.scalar.copy)
+                evac(NT - 6, 2, nc.scalar.copy)
             if 0 <= s - 4 < NT:
                 expo(s - 4)
             je = s - LAG - 3
-            if je >= 1 and je % 2 == 1 and je < NT:
-                evac(je // 2)
+            if je >= 1 and je % 2 == 1 and je < NT - 8:
+                evac(je - 1, 2, nc.scalar.copy)
             if s < NT:
                 prod_s(s)
             if 0 <= s - 2 <= NT:
                 slot(s - 2)
-            elif NT < s - 2 < NT + LAG:
-                mx_pass(s - 2 - LAG)
+            elif s - 2 > NT:
+                results(s - 2)
+            if s == NT + 5:
+                evac(NT - 4, 2, nc.vector.tensor_copy)
+                evac(NT - 2, 1, nc.vector.tensor_copy)
+            if s == NT + 6:
+                evac(NT - 1, 1, nc.scalar.copy)

@@ -21,18 +21,18 @@ BIG = 3.0e38
 FLOPS = 2 * N * M * POUT
 
 NG = 3
-NS = 6
-V0 = NG + NS
+NS = 5
+V0 = NG + 1 + NS
+PATTERN = "GS"
 NV = D - V0
-NADD = 1
-EVA = 2
-EVB = 2
+NADD = 0
+EVB = 3
 QG = 4
 LAG = 7
 C0 = 8
 NWARM = 5
 LO = 4
-FIRST_EV = 3
+FIRST_EV = 1
 
 
 def q_group(i):
@@ -104,7 +104,7 @@ def tile_tmk_t_kernel(tc, x, design_points, chol_inv, out):
         xn = const.tile([P, NT, D], F32)
         s_all = const.tile([P, PACK], F32)
         s_sc = const.tile([P, PACK], F32)
-        cz = const.tile([P, PACK], F32)
+        cz = const.tile([P, 2, PACK], F32)
 
         def wide(t, a, b):
             return t[:, a:b].unsqueeze(2).to_broadcast([P, b - a, D])
@@ -128,11 +128,12 @@ def tile_tmk_t_kernel(tc, x, design_points, chol_inv, out):
         ln_sum(0, C0)
         nc.vector.tensor_reduce(out=s_all[:], in_=z_sb[:], axis=AX.X, op=ALU.add)
         nc.vector.scalar_tensor_tensor(out=xc[:, 0:C0, :], in0=wide(sm, 0, C0), scalar=-1.0 / D, in1=x_sb[:, 0:C0, :], op0=ALU.mult, op1=ALU.add)
-        nc.vector.tensor_reduce(out=s_sc[:], in_=z_sb[:, :, NG:V0], axis=AX.X, op=ALU.add)
+        nc.vector.tensor_reduce(out=s_sc[:], in_=z_sb[:, :, NG + 1:V0], axis=AX.X, op=ALU.add)
         nc.vector.tensor_tensor(out=sq[:, 0:C0, :], in0=xc[:, 0:C0, :], in1=xc[:, 0:C0, :], op=ALU.mult)
-        nc.vector.scalar_tensor_tensor(out=cz[:], in0=s_all[:], scalar=-0.5, in1=s_sc[:], op0=ALU.mult, op1=ALU.add)
+        nc.vector.scalar_tensor_tensor(out=cz[:, 0, :], in0=s_all[:], scalar=-0.5, in1=s_sc[:], op0=ALU.mult, op1=ALU.add)
         ln_var(0, C0)
         ln_sqrt(0, C0)
+        nc.vector.tensor_tensor(out=cz[:, 1, :], in0=cz[:, 0, :], in1=z_sb[:, :, NG], op=ALU.add)
         ln_rs(0, C0)
         nc.vector.tensor_tensor(out=xn[:, 0:C0, :], in0=xc[:, 0:C0, :], in1=wide(rs, 0, C0), op=ALU.mult)
         ln_sum(C0, NT)
@@ -175,13 +176,19 @@ def tile_tmk_t_kernel(tc, x, design_points, chol_inv, out):
             for h in range(min(2, NV - 2 * b)):
                 spread(zp, V0 + 2 * b + h, h)
 
-        cp = psa.tile([P, M], F32, tag="acc", name="cp")
-        c_sb = const.tile([P, M], F32)
+        c_sb = {}
+
+        def need_c(v):
+            cp = psa.tile([P, M], F32, tag="acc", name="cp")
+            for t in range(PACK):
+                nc.tensor.transpose(cp[:, t * P:(t + 1) * P], cz[:, v, t:t + 1].to_broadcast([P, P]), ident_f[:])
+            c_sb[v] = const.tile([P, M], F32, name="c_sb%d" % v)
+            nc.scalar.copy(out=c_sb[v][:], in_=cp[:])
+
         need_zp(0)
-        for t in range(PACK):
-            nc.tensor.transpose(cp[:, t * P:(t + 1) * P], cz[:, t:t + 1].to_broadcast([P, P]), ident_f[:])
-        nc.scalar.copy(out=c_sb[:], in_=cp[:])
+        need_c(0)
         need_zp(2)
+        need_c(1)
 
         out_v = out.rearrange("(p i) c -> p i c", i=NT)
 
@@ -193,18 +200,27 @@ def tile_tmk_t_kernel(tc, x, design_points, chol_inv, out):
         cq_of = {}
         ops_of = {}
 
+        def s_takes(i):
+            return PATTERN[i % len(PATTERN)] == "S"
+
+        def n_s(i):
+            return NS + (1 if s_takes(i) else 0)
+
+        def n_g(i):
+            return NG + (0 if s_takes(i) else 1)
+
         def prod_s(i):
-            ts = tsp.tile([P, NS, M], F32, name="ts")
+            ts = tsp.tile([P, NS + 1, M], F32, name="ts")
             ts_of[i] = ts
-            for k in range(NS):
-                d = NG + k
+            for k in range(n_s(i)):
+                d = NG + 1 + k if k < NS else NG
                 need_zb(d)
                 nc.scalar.activation(out=ts[:, k, :], in_=zb[:, d, :], func=ACT.Relu, bias=xn[:, i, d:d + 1], scale=-1.0)
 
         def prod_g(i):
-            tg = tgp.tile([P, NG, M], F32, name="tg")
+            tg = tgp.tile([P, NG + 1, M], F32, name="tg")
             tg_of[i] = tg
-            for d in range(NG):
+            for d in range(n_g(i)):
                 need_zb(d)
                 nc.gpsimd.tensor_scalar(out=tg[:, d, :], in0=zb[:, d, :], scalar1=BIG, scalar2=xn[:, i, d:d + 1], op0=ALU.min, op1=ALU.max)
 
@@ -219,7 +235,7 @@ def tile_tmk_t_kernel(tc, x, design_points, chol_inv, out):
             need_zp(k)
             tv = tv_of[i]
             table = zps[k // 2][:, (k % 2) * M:(k % 2 + 1) * M]
-            prev = c_sb if k == 0 else tv
+            prev = c_sb[1 if s_takes(i) else 0] if k == 0 else tv
             nc.vector.scalar_tensor_tensor(
                 out=tv[:], in0=table, scalar=xn[:, i, V0 + k:V0 + k + 1], in1=prev[:], op0=ALU.max, op1=ALU.add)
 
@@ -250,8 +266,8 @@ def tile_tmk_t_kernel(tc, x, design_points, chol_inv, out):
 
         def terms_of(i):
             ts = ts_of[i]
-            terms = [ts[:, k, :] for k in range(2 * NADD, NS)]
-            terms += [tg_of[i][:, k, :] for k in range(NG)]
+            terms = [ts[:, k, :] for k in range(2 * NADD, n_s(i))]
+            terms += [tg_of[i][:, k, :] for k in range(n_g(i))]
             terms += [ts[:, 2 * a, :] for a in range(NADD)]
             terms.append(tv_of[i][:])
             return terms
@@ -259,9 +275,6 @@ def tile_tmk_t_kernel(tc, x, design_points, chol_inv, out):
         def slot(i):
             if i < NT:
                 acc_of[i] = psa.tile([P, M], F32, tag="acc", name="acc")
-                if FIRST_EV <= i < NT - 1:
-                    for r in range(EVA):
-                        mx(i - LAG, acc_of[i][:, 0:POUT])
             for h in range(2):
                 jobs = []
                 if i >= 1:
@@ -315,6 +328,7 @@ def tile_tmk_t_kernel(tc, x, design_points, chol_inv, out):
                 ln_var(C0, NT)
             if s == 2:
                 ln_rs(C0, NT)
+            if s == 1:
                 nc.vector.quantize_mx(out=w_codes[:].bitcast(FP8X4), scales=w_scl[:], in_=w_grp[:].rearrange("p w j -> p (w j)"))
             iq = s - 5
             if 0 <= iq < NT and iq == sum(q_group(iq)) - 1:

from contextlib import ExitStack

import concourse.mybir as mybir
from concourse.masks import make_identity

F32 = mybir.dt.float32
BF16 = mybir.dt.bfloat16
U32 = mybir.dt.uint32
U8 = mybir.dt.uint8
FP8X4 = mybir.dt.float8_e4m3fn_x4
ALU = mybir.AluOpType
ACT = mybir.ActivationFunctionType
AX = mybir.AxisListType

N, M, POUT, D = 8192, 512, 256, 16
P = 128
NT = N // P
PACK = 4
LN_EPS = 1e-5
BIG = 3.0e38
FLOPS = 2 * N * M * POUT

NG = 3
NS = 5
V0 = NG + 1 + NS
PATTERN = "GS"
NV = D - V0
NADD = 0
EVB = 3
QG = 4
LAG = 7
C0 = 8
NWARM = 5
LO = 4
FIRST_EV = 1


def q_group(i):
    if i >= NT - QG:
        if i < NT - 2:
            return NT - QG, 2
        return i, 1
    return i - i % QG, QG


def result_slot(j):
    if j >= NT - 2:
        return j + 4
    if j >= NT - 4:
        return NT + 1
    if j >= NT - 8:
        return NT - 1
    return j + LAG


def tile_tmk_t_kernel(tc, x, design_points, chol_inv, out):
    nc = tc.nc
    with ExitStack() as ctx:
        ctx.enter_context(tc.manual_schedule())
        const = ctx.enter_context(tc.tile_pool(name="const", bufs=1))
        tsp = ctx.enter_context(tc.tile_pool(name="tsp", bufs=5))
        tgp = ctx.enter_context(tc.tile_pool(name="tgp", bufs=5))
        tvp = ctx.enter_context(tc.tile_pool(name="tvp", bufs=5))
        kqp = ctx.enter_context(tc.tile_pool(name="kqp", bufs=4))
        cqp = ctx.enter_context(tc.tile_pool(name="cqp", bufs=5))
        osp = ctx.enter_context(tc.tile_pool(name="osp", bufs=4))
        psz = ctx.enter_context(tc.psum_pool(name="psz", bufs=1))
        psa = ctx.enter_context(tc.psum_pool(name="psa", bufs=3))
        pso = ctx.enter_context(tc.psum_pool(name="pso", bufs=1))

        x_v = x.rearrange("(p i) d -> p i d", i=NT)
        x_sb = const.tile([P, NT, D], BF16)
        nc.sync.dma_start(out=x_sb[:, 0:C0, :], in_=x_v[:, 0:C0, :])
        z_sb = const.tile([P, PACK, D], BF16)
        nc.scalar.dma_start(out=z_sb[:], in_=design_points.rearrange("(p t) d -> p t d", t=PACK))
        nc.sync.dma_start(out=x_sb[:, C0:NT, :], in_=x_v[:, C0:NT, :])
        w_raw = const.tile([P, PACK, POUT], BF16)
        nc.sync.dma_start(out=w_raw[:], in_=chol_inv.rearrange("(p j) w -> p j w", j=PACK))

        one = const.tile([P, 1], F32)
        nc.vector.memset(one[:], 1.0)
        one2 = const.tile([P, 1], F32)
        nc.scalar.activation(out=one2[:], in_=one[:], func=ACT.Sqrt)

        ident_b = const.tile([P, P], BF16)
        make_identity(nc, ident_b[:])
        ident_f = const.tile([P, P], F32)
        make_identity(nc, ident_f[:])

        wz = const.tile([P, M], BF16)
        nc.vector.memset(wz[:], 0.0)
        wp = psa.tile([P, M], F32, tag="acc", name="wp")
        for r in range(NWARM):
            nc.tensor.matmul(out=wp[:], lhsT=wz[:, 0:P], rhs=wz[:], start=True, stop=True)

        sm = const.tile([P, NT], F32)
        xc = const.tile([P, NT, D], F32)
        sq = const.tile([P, NT, D], F32)
        ss = const.tile([P, NT], F32)
        ve = const.tile([P, NT], F32)
        sd = const.tile([P, NT], F32)
        rs = const.tile([P, NT], F32)
        nw = const.tile([P, NT], F32)
        xn = const.tile([P, NT, D], F32)
        s_all = const.tile([P, PACK], F32)
        s_sc = const.tile([P, PACK], F32)
        cz = const.tile([P, 2, PACK], F32)

        def wide(t, a, b):
            return t[:, a:b].unsqueeze(2).to_broadcast([P, b - a, D])

        def ln_sum(a, b):
            nc.vector.tensor_reduce(out=sm[:, a:b], in_=x_sb[:, a:b, :], axis=AX.X, op=ALU.add)

        def ln_var(a, b):
            nc.vector.tensor_reduce(out=ss[:, a:b], in_=sq[:, a:b, :], axis=AX.X, op=ALU.add)
            nc.vector.tensor_scalar(out=ve[:, a:b], in0=ss[:, a:b], scalar1=1.0 / D, scalar2=LN_EPS, op0=ALU.mult, op1=ALU.add)

        def ln_sqrt(a, b):
            nc.scalar.activation(out=sd[:, a:b], in_=ve[:, a:b], func=ACT.Sqrt)

        def ln_rs(a, b):
            nc.vector.reciprocal(out=rs[:, a:b], in_=sd[:, a:b])
            nc.vector.tensor_tensor(out=nw[:, a:b], in0=rs[:, a:b], in1=rs[:, a:b], op=ALU.mult)
            nc.vector.scalar_tensor_tensor(out=nw[:, a:b], in0=nw[:, a:b], scalar=-0.5, in1=ve[:, a:b], op0=ALU.mult, op1=ALU.mult)
            nc.vector.scalar_tensor_tensor(out=rs[:, a:b], in0=nw[:, a:b], scalar=1.5, in1=rs[:, a:b], op0=ALU.add, op1=ALU.mult)

        ln_sum(0, C0)
        nc.vector.tensor_reduce(out=s_all[:], in_=z_sb[:], axis=AX.X, op=ALU.add)
        nc.vector.scalar_tensor_tensor(out=xc[:, 0:C0, :], in0=wide(sm, 0, C0), scalar=-1.0 / D, in1=x_sb[:, 0:C0, :], op0=ALU.mult, op1=ALU.add)
        nc.vector.tensor_reduce(out=s_sc[:], in_=z_sb[:, :, NG + 1:V0], axis=AX.X, op=ALU.add)
        nc.vector.tensor_tensor(out=sq[:, 0:C0, :], in0=xc[:, 0:C0, :], in1=xc[:, 0:C0, :], op=ALU.mult)
        nc.vector.scalar_tensor_tensor(out=cz[:, 0, :], in0=s_all[:], scalar=-0.5, in1=s_sc[:], op0=ALU.mult, op1=ALU.add)
        ln_var(0, C0)
        ln_sqrt(0, C0)
        nc.vector.tensor_tensor(out=cz[:, 1, :], in0=cz[:, 0, :], in1=z_sb[:, :, NG], op=ALU.add)
        ln_rs(0, C0)
        nc.vector.tensor_tensor(out=xn[:, 0:C0, :], in0=xc[:, 0:C0, :], in1=wide(rs, 0, C0), op=ALU.mult)
        ln_sum(C0, NT)
        nc.vector.tensor_scalar(out=sm[:, C0:NT], in0=sm[:, C0:NT], scalar1=1.0 / D, scalar2=None, op0=ALU.mult)

        w_grp = const.tile([P, POUT, PACK], BF16, align_bytes=64)
        w_codes = const.tile([P, POUT], U32, align_bytes=64)
        w_scl = const.tile([P, POUT], U8, align_bytes=64)
        nc.gpsimd.tensor_scalar(out=w_grp[:], in0=w_raw[:].rearrange("p j w -> p w j"), scalar1=1.0, scalar2=0.0, op0=ALU.mult, op1=ALU.add)
        nc.gpsimd.tensor_tensor(out=xc[:, C0:NT, :], in0=x_sb[:, C0:NT, :], in1=wide(sm, C0, NT), op=ALU.subtract)
        nc.gpsimd.tensor_tensor(out=sq[:, C0:NT, :], in0=xc[:, C0:NT, :], in1=xc[:, C0:NT, :], op=ALU.mult)

        def spread(dst, d, h):
            for t in range(PACK):
                c0 = h * M + t * P
                nc.tensor.transpose(dst[:, c0:c0 + P], z_sb[:, t, d:d + 1].to_broadcast([P, P]), ident_b[:])

        zb = const.tile([P, V0 + V0 % 2, M], BF16)
        zb_made = set()

        def need_zb(d):
            pair = d // 2
            if pair in zb_made:
                return
            zb_made.add(pair)
            nh = min(2, V0 - 2 * pair)
            tp = psa.tile([P, 2 * M], BF16, tag="acc", name="tp")
            for h in range(nh):
                spread(tp, 2 * pair + h, h)
            nc.scalar.copy(out=zb[:, 2 * pair:2 * pair + nh, :], in_=tp[:, 0:nh * M].rearrange("p (h m) -> p h m", h=nh))

        zps = {}

        def need_zp(k):
            b = k // 2
            if b in zps:
                return
            zp = psz.tile([P, 2 * M], BF16, name="zp%d" % b)
            zps[b] = zp
            for h in range(min(2, NV - 2 * b)):
                spread(zp, V0 + 2 * b + h, h)

        c_sb = {}

        def need_c(v):
            cp = psa.tile([P, M], F32, tag="acc", name="cp")
            for t in range(PACK):
                nc.tensor.transpose(cp[:, t * P:(t + 1) * P], cz[:, v, t:t + 1].to_broadcast([P, P]), ident_f[:])
            c_sb[v] = const.tile([P, M], F32, name="c_sb%d" % v)
            nc.scalar.copy(out=c_sb[v][:], in_=cp[:])

        need_zp(0)
        need_c(0)
        need_zp(2)
        need_c(1)

        out_v = out.rearrange("(p i) c -> p i c", i=NT)

        ts_of = {}
        tg_of = {}
        tv_of = {}
        acc_of = {}
        kq_of = {}
        cq_of = {}
        ops_of = {}

        def s_takes(i):
            return PATTERN[i % len(PATTERN)] == "S"

        def n_s(i):
            return NS + (1 if s_takes(i) else 0)

        def n_g(i):
            return NG + (0 if s_takes(i) else 1)

        def prod_s(i):
            ts = tsp.tile([P, NS + 1, M], F32, name="ts")
            ts_of[i] = ts
            for k in range(n_s(i)):
                d = NG + 1 + k if k < NS else NG
                need_zb(d)
                nc.scalar.activation(out=ts[:, k, :], in_=zb[:, d, :], func=ACT.Relu, bias=xn[:, i, d:d + 1], scale=-1.0)

        def prod_g(i):
            tg = tgp.tile([P, NG + 1, M], F32, name="tg")
            tg_of[i] = tg
            for d in range(n_g(i)):
                need_zb(d)
                nc.gpsimd.tensor_scalar(out=tg[:, d, :], in0=zb[:, d, :], scalar1=BIG, scalar2=xn[:, i, d:d + 1], op0=ALU.min, op1=ALU.max)

        def add_g(i):
            ts = ts_of[i]
            for a in range(NADD):
                nc.gpsimd.tensor_tensor(out=ts[:, 2 * a, :], in0=ts[:, 2 * a, :], in1=ts[:, 2 * a + 1, :], op=ALU.add)

        def chain_v(i, k):
            if k == 0:
                tv_of[i] = tvp.tile([P, M], F32, name="tv")
            need_zp(k)
            tv = tv_of[i]
            table = zps[k // 2][:, (k % 2) * M:(k % 2 + 1) * M]
            prev = c_sb[1 if s_takes(i) else 0] if k == 0 else tv
            nc.vector.scalar_tensor_tensor(
                out=tv[:], in0=table, scalar=xn[:, i, V0 + k:V0 + k + 1], in1=prev[:], op0=ALU.max, op1=ALU.add)

        def ops_place(j):
            if j >= NT - 2:
                return j - NT // 2 + 1, 0
            return j // 2, j % 2

        def mx(j, dst):
            if j < 0:
                lhs, lhs_s = w_codes[:, 0:P], w_scl[:, 0:P]
            else:
                codes, scl = cq_of[q_group(j)[0]]
                r = j - q_group(j)[0]
                lhs, lhs_s = codes[:, r * P:(r + 1) * P], scl[:, r * P:(r + 1) * P]
            nc.tensor.matmul_mx(
                out=dst, lhsT=lhs.bitcast(FP8X4), lhsT_scale=lhs_s,
                rhs=w_codes[:].bitcast(FP8X4), rhs_scale=w_scl[:], start=True, stop=True)

        def result(j):
            g, e = ops_place(j)
            if g not in ops_of:
                if j >= NT - 2 or NT - 6 <= j < NT - 4:
                    ops_of[g] = psa.tile([P, 2 * POUT], F32, tag="acc", name="ops_end")
                else:
                    ops_of[g] = pso.tile([P, 2 * POUT], F32, name="ops")
            mx(j, ops_of[g][:, e * POUT:(e + 1) * POUT])

        def terms_of(i):
            ts = ts_of[i]
            terms = [ts[:, k, :] for k in range(2 * NADD, n_s(i))]
            terms += [tg_of[i][:, k, :] for k in range(n_g(i))]
            terms += [ts[:, 2 * a, :] for a in range(NADD)]
            terms.append(tv_of[i][:])
            return terms

        def slot(i):
            if i < NT:
                acc_of[i] = psa.tile([P, M], F32, tag="acc", name="acc")
            for h in range(2):
                jobs = []
                if i >= 1:
                    jobs.append((acc_of[i - 1], 2 + h, terms_of(i - 1)))
                if i < NT:
                    jobs.append((acc_of[i], h, terms_of(i)))
                for q in range(max(len(job[2]) for job in jobs)):
                    for acc, t, terms in jobs:
                        nc.tensor.matmul(
                            out=acc[:, t * P:(t + 1) * P], lhsT=terms[q][:, t * P:(t + 1) * P], rhs=ident_f[:],
                            is_transpose=True, start=(q == 0), stop=(q == len(terms) - 1))
                if h == 0:
                    results(i)

        def results(i):
            made = [j for j in range(max(0, i - LAG), NT) if result_slot(j) == i]
            for j in made:
                result(j)
            if FIRST_EV <= i < NT - 1:
                for r in range(EVB - len(made)):
                    g, e = ops_place(max(0, i - LAG))
                    if g not in ops_of:
                        ops_of[g] = pso.tile([P, 2 * POUT], F32, name="ops")
                    mx(i - LAG, ops_of[g][:, e * POUT:(e + 1) * POUT])

        def expo(i):
            a, n = q_group(i)
            if i == a:
                kq_of[a] = kqp.tile([P, QG, M], BF16, align_bytes=64, name="kq")
            kq = kq_of[a]
            nc.scalar.activation(
                out=kq[:, i - a, :].rearrange("p (n t) -> p n t", t=PACK),
                in_=acc_of[i][:].rearrange("p (t n) -> p n t", t=PACK), func=ACT.Exp, scale=-2.0)

        def quant(a, n):
            codes = cqp.tile([P, QG * P], U32, align_bytes=64, name="codes")
            scl = cqp.tile([P, QG * P], U8, align_bytes=64, name="scl")
            cq_of[a] = (codes, scl)
            nc.vector.quantize_mx(
                out=codes[:, 0:n * P].bitcast(FP8X4), scales=scl[:, 0:n * P],
                in_=kq_of[a][:, 0:n, :].rearrange("p g m -> p (g m)"))

        def evac(j0, n, copy):
            o_sb = osp.tile([P, 2, POUT], F32, name="o_sb")
            src = ops_of[ops_place(j0)[0]][:, 0:n * POUT]
            copy(out=o_sb[:, 0:n, :], in_=src.rearrange("p (e c) -> p e c", e=n))
            nc.sync.dma_start(out=out_v[:, j0:j0 + n, :], in_=o_sb[:, 0:n, :])

        for s in range(NT + 7):
            if s == 1:
                ln_var(C0, NT)
            if s == 2:
                ln_rs(C0, NT)
            if s == 1:
                nc.vector.quantize_mx(out=w_codes[:].bitcast(FP8X4), scales=w_scl[:], in_=w_grp[:].rearrange("p w j -> p (w j)"))
            iq = s - 5
            if 0 <= iq < NT and iq == sum(q_group(iq)) - 1:
                quant(q_group(iq)[0], q_group(iq)[1])
            for k in range(max(LO, NV - LO)):
                if s < NT and k < LO:
                    chain_v(s, k)
                if 0 <= s - 1 < NT and LO + k < NV:
                    chain_v(s - 1, LO + k)
            if s == 2:
                nc.gpsimd.tensor_tensor(out=xn[:, C0:NT, :], in0=xc[:, C0:NT, :], in1=wide(rs, C0, NT), op=ALU.mult)
            if 0 <= s - 1 < NT:
                add_g(s - 1)
            if s < NT:
                prod_g(s)
            if s == 1:
                ln_sqrt(C0, NT)
            if s == NT + 2:
                evac(NT - 8, 2, nc.scalar.copy)
                evac(NT - 6, 2, nc.scalar.copy)
            if 0 <= s - 4 < NT:
                expo(s - 4)
            je = s - LAG - 3
            if je >= 1 and je % 2 == 1 and je < NT - 8:
                evac(je - 1, 2, nc.scalar.copy)
            if s < NT:
                prod_s(s)
            if 0 <= s - 2 <= NT:
                slot(s - 2)
            elif s - 2 > NT:
                results(s - 2)
            if s == NT + 5:
                evac(NT - 4, 2, nc.vector.tensor_copy)
                evac(NT - 2, 1, nc.vector.tensor_copy)
            if s == NT + 6:
                evac(NT - 1, 1, nc.scalar.copy)
